import numpy as np
import ml_dtypes


def mxq(x, axis, fmt="e4m3"):
    dtype, down = {"e4m3": (ml_dtypes.float8_e4m3fn, 7), "e5m2": (ml_dtypes.float8_e5m2, 14)}[fmt]
    v = np.moveaxis(np.asarray(x, np.float32).astype(ml_dtypes.bfloat16).astype(np.float64), axis, -1)
    blocks = v.reshape(v.shape[:-1] + (-1, 32))
    amax = np.abs(blocks).max(-1, keepdims=True)
    byte = np.maximum(np.where(amax > 0, np.frexp(amax)[1] - 1 + 127, 0) - down, 1)
    scale = np.exp2(byte - 127.0)
    codes = (blocks / scale).astype(np.float32).astype(dtype).astype(np.float64)
    return np.moveaxis((codes * scale).reshape(v.shape), -1, axis)


WIDE = False


def mx_kscale(k):
    if not WIDE:
        return np.ones(k)
    levels = np.array([10, -10, 5, -5, 0])
    if k % 512:
        return np.exp2(np.random.permutation(np.resize(levels, k // 32))).repeat(32)
    a = np.empty((k // 512, 16))
    for p in range(k // 512):
        a[p, :8] = np.random.permutation(np.resize(levels, 8))
        for g in range(8):
            far = levels[np.abs(levels - a[p, g]) >= 10]
            a[p, g + 8] = far[np.random.randint(len(far))]
    return np.exp2(a.ravel()).repeat(32)


BF16 = ml_dtypes.bfloat16


def bf(x):
    return np.asarray(x, np.float32).astype(BF16)


def f64(x):
    return np.asarray(x).astype(np.float64)


B, S, H, DH, C = 2, 1024, 2048, 256, 512
SCALE_BASE = 2.0 ** 9


def rotate_every_two(y):
    y1 = y[..., ::2]
    y2 = y[..., 1::2]
    return np.stack((-y2, y1), axis=-1).reshape(y.shape)


def xpos(y, downscale):
    L, D = y.shape[-2], y.shape[-1]
    d = D // 2
    scale_vec = (np.arange(0, D, 2) + 0.4 * D) / (1.4 * D)
    min_pos = (-L) // 2
    power = np.arange(min_pos, L + min_pos) / SCALE_BASE
    scale = scale_vec ** power[:, None]
    inv_freq = 1.0 / (10000.0 ** (np.arange(d) / d))
    sinusoid = np.arange(L)[:, None] * inv_freq
    sin, cos = np.sin(sinusoid), np.cos(sinusoid)
    if downscale:
        scale = 1.0 / scale
    sin = np.repeat(sin * scale, 2, axis=-1)
    cos = np.repeat(cos * scale, 2, axis=-1)
    return y * cos + rotate_every_two(y) * sin


def setup_inputs():
    s = mx_kscale(H)
    return {"x": bf(np.random.standard_normal((B, S, H)) * s),
            "w_q": bf(np.random.standard_normal((H, DH)) * 0.5 / np.sqrt(H) / s[:, None]),
            "w_k": bf(np.random.standard_normal((H, DH)) * 0.5 / np.sqrt(H) / s[:, None]),
            "w_v": bf(np.random.standard_normal((H, DH)) * 0.25 / np.sqrt(H) / s[:, None])}


def reference(x, w_q, w_k, w_v):
    xq = mxq(f64(x), 2, "e4m3")
    q = xpos(xq @ mxq(f64(w_q), 0, "e4m3"), False)
    k = xpos(xq @ mxq(f64(w_k), 0, "e4m3"), True)
    v = xq @ mxq(f64(w_v), 0, "e4m3")
    return q, k, v

@@ -1,0 +1,320 @@
+from contextlib import ExitStack
+import math
+
+import concourse.mybir as mybir
+from concourse.masks import make_identity
+
+F32 = mybir.dt.float32
+BF16 = mybir.dt.bfloat16
+I32 = mybir.dt.int32
+U32 = mybir.dt.uint32
+U8 = mybir.dt.uint8
+FP8X4 = mybir.dt.float8_e4m3fn_x4
+ALU = mybir.AluOpType
+ACT = mybir.ActivationFunctionType
+
+P = 128
+BATCH, SEQ, HID, DH = 2, 1024, 2048, 256
+PAIRS = DH // 2
+TILES = SEQ // P
+PACK = 4
+PASSES = HID // (P * PACK)
+WORDS = HID // 2
+ROUND = 2
+ROUNDS = BATCH * TILES // ROUND
+AHEAD = 5
+
+ROTARY_BASE = 10000.0
+SCALE_BASE = 512.0
+ROUND_MAGIC = 1.5 * 2.0**23
+
+FLOPS = 2 * BATCH * SEQ * HID * 3 * DH
+
+
+def tile_retblock_pa_kernel(tc, x, w_q, w_k, w_v, out_0, out_1, out_2):
+    nc = tc.nc
+    with ExitStack() as ctx:
+        const = ctx.enter_context(tc.tile_pool(name="const", bufs=1))
+        x_raw_pool = ctx.enter_context(tc.tile_pool(name="x_raw_pool", bufs=AHEAD))
+        x_mx_pool = ctx.enter_context(tc.tile_pool(name="x_mx_pool", bufs=3))
+        w_grouped_pool = ctx.enter_context(tc.tile_pool(name="w_grouped_pool", bufs=2))
+        work = ctx.enter_context(tc.tile_pool(name="work", bufs=3))
+        xt_psum = ctx.enter_context(tc.psum_pool(name="xt_psum", bufs=4))
+        qk_psum = ctx.enter_context(tc.psum_pool(name="qk_psum", bufs=3))
+        v_psum = ctx.enter_context(tc.psum_pool(name="v_psum", bufs=1))
+        ctx.enter_context(tc.manual_schedule())
+
+        def batch_of(r):
+            return r % BATCH
+
+        def first_tile_of(r):
+            return (r // BATCH) * ROUND
+
+        def load_x(r):
+            x_raw = x_raw_pool.tile([P, ROUND * HID], BF16, name="x_raw")
+            rows = x[batch_of(r)].rearrange("(p t) k -> p (t k)", t=TILES)
+            first = first_tile_of(r) * HID
+            nc.sync.dma_start(out=x_raw[:], in_=rows[:, first : first + ROUND * HID])
+            return x_raw
+
+        def load_w(w, name):
+            w_raw = const.tile([P, PASSES * PACK, DH], BF16, name=name)
+            nc.sync.dma_start(
+                out=w_raw[:].rearrange("p (g t) c -> p g (t c)", t=PACK),
+                in_=w.rearrange("(g p t) c -> p g (t c)", p=P, t=PACK),
+            )
+            return w_raw
+
+        def regroup_w(w_raw):
+            w_grouped = w_grouped_pool.tile(
+                [P, PASSES, DH, PACK], BF16, align_bytes=64, name="w_grouped"
+            )
+            for g in range(PASSES):
+                nc.vector.tensor_copy(
+                    out=w_grouped[:, g].rearrange("p (c i) t -> p c t i", i=4),
+                    in_=w_raw[:, g * PACK : (g + 1) * PACK, :].rearrange(
+                        "p t (c i) -> p c t i", i=4
+                    ),
+                )
+            return w_grouped
+
+        def quantise_w(w_grouped, name):
+            codes = const.tile([P, PASSES * DH], U32, align_bytes=64, name=name + "_codes")
+            scales = const.tile([P, PASSES * DH], U8, align_bytes=64, name=name + "_scales")
+            nc.vector.quantize_mx(
+                out=codes[:].bitcast(FP8X4),
+                scales=scales[:],
+                in_=w_grouped[:].rearrange("p g c t -> p (g c t)"),
+            )
+            return codes, scales
+
+        def transpose_x(x_raw):
+            words = x_raw[:].bitcast(F32)
+            x_grouped = x_mx_pool.tile([P, ROUND * HID], BF16, align_bytes=64, name="x_grouped")
+            grouped_words = x_grouped[:].bitcast(F32)
+            for bank in range(ROUND * WORDS // (4 * P)):
+                xt = xt_psum.tile([P, 4, P], F32, name="xt")
+                for a in range(4):
+                    start = (bank * 2 + a // 2) * 2 * P
+                    nc.tensor.transpose(
+                        xt[:, a, :], words[:, start + a % 2 : start + 2 * P : 2], ident[:]
+                    )
+                first = bank * 4 * P
+                nc.scalar.copy(
+                    out=grouped_words[:, first : first + 4 * P].rearrange(
+                        "p (g r u) -> p g r u", g=2, u=2
+                    ),
+                    in_=xt[:].rearrange("p (g u) r -> p g r u", u=2),
+                )
+            return x_grouped
+
+        def quantise_x(x_grouped):
+            codes = x_mx_pool.tile([P, ROUND * PASSES * P], U32, align_bytes=64, name="x_codes")
+            scales = x_mx_pool.tile([P, ROUND * PASSES * P], U8, align_bytes=64, name="x_scales")
+            for i in range(ROUND):
+                cols = slice(i * PASSES * P, (i + 1) * PASSES * P)
+                nc.vector.quantize_mx(
+                    out=codes[:, cols].bitcast(FP8X4),
+                    scales=scales[:, cols],
+                    in_=x_grouped[:, i * HID : (i + 1) * HID],
+                )
+            return codes, scales
+
+        def project(out, x_mx, i, w_mx):
+            x_codes, x_scales = x_mx
+            w_codes, w_scales = w_mx
+            for g in range(PASSES):
+                tokens = slice((i * PASSES + g) * P, (i * PASSES + g + 1) * P)
+                features = slice(g * DH, (g + 1) * DH)
+                nc.tensor.matmul_mx(
+                    out=out,
+                    lhsT=x_codes[:, tokens].bitcast(FP8X4),
+                    lhsT_scale=x_scales[:, tokens],
+                    rhs=w_codes[:, features].bitcast(FP8X4),
+                    rhs_scale=w_scales[:, features],
+                    start=(g == 0),
+                    stop=(g == PASSES - 1),
+                )
+
+        plain = [P, TILES, PAIRS]
+        both = [P, TILES, 2, PAIRS]
+        angle = const.tile(plain, F32, name="angle")
+        zoom = const.tile(both, F32, name="zoom")
+        sine = const.tile(plain, F32, name="sine")
+        cosine = const.tile(plain, F32, name="cosine")
+        cos_tab = const.tile(both, F32, name="cos_tab")
+        sin_tab = const.tile(both, F32, name="sin_tab")
+
+        def table_columns():
+            j_int = const.tile([P, PAIRS], I32, name="j_int")
+            nc.gpsimd.iota(j_int[:], pattern=[[1, PAIRS]], base=0, channel_multiplier=0)
+            pos_int = const.tile([P, TILES], I32, name="pos_int")
+            nc.gpsimd.iota(pos_int[:], pattern=[[1, TILES]], base=0, channel_multiplier=TILES)
+            log_base = const.tile([P, PAIRS], F32, name="log_base")
+            nc.vector.tensor_copy(out=log_base[:], in_=j_int[:])
+            nc.vector.tensor_scalar(
+                out=log_base[:], in0=log_base[:], scalar1=2.0 / (1.4 * DH), scalar2=0.4 / 1.4,
+                op0=ALU.mult, op1=ALU.add,
+            )
+            nc.scalar.activation(out=log_base[:], in_=log_base[:], func=ACT.Ln)
+            pos = const.tile([P, TILES], F32, name="pos")
+            nc.vector.tensor_copy(out=pos[:], in_=pos_int[:])
+            centred = const.tile([P, TILES], F32, name="centred")
+            nc.vector.tensor_scalar(
+                out=centred[:], in0=pos[:], scalar1=float(SEQ // 2), scalar2=1.0 / SCALE_BASE,
+                op0=ALU.subtract, op1=ALU.mult,
+            )
+            pos_turns = const.tile([P, TILES], F32, name="pos_turns")
+            nc.vector.tensor_scalar(
+                out=pos_turns[:], in0=pos[:], scalar1=1.0 / (2.0 * math.pi), scalar2=None,
+                op0=ALU.mult,
+            )
+            freq = const.tile([P, PAIRS], F32, name="freq")
+            nc.vector.memset(freq[:, 0:1], 1.0)
+            for doubling in range(7):
+                width = 2**doubling
+                nc.vector.tensor_scalar(
+                    out=freq[:, width : 2 * width], in0=freq[:, 0:width],
+                    scalar1=ROTARY_BASE ** (-width / PAIRS), scalar2=None, op0=ALU.mult,
+                )
+            return log_base, centred, pos_turns, freq
+
+        def table_zoom(log_base, centred):
+            log_z = const.tile(plain, F32, name="log_z")
+            nc.vector.tensor_tensor(
+                out=log_z[:],
+                in0=centred[:].unsqueeze(2).to_broadcast(plain),
+                in1=log_base[:].unsqueeze(1).to_broadcast(plain),
+                op=ALU.mult,
+            )
+            nc.scalar.activation(out=zoom[:, :, 0, :], in_=log_z[:], func=ACT.Exp)
+            nc.scalar.activation(out=zoom[:, :, 1, :], in_=log_z[:], func=ACT.Exp, scale=-1.0)
+
+        def table_turns(pos_turns, freq):
+            nc.vector.tensor_tensor(
+                out=angle[:],
+                in0=pos_turns[:].unsqueeze(2).to_broadcast(plain),
+                in1=freq[:].unsqueeze(1).to_broadcast(plain),
+                op=ALU.mult,
+            )
+
+        def table_fraction():
+            whole = const.tile(plain, F32, name="whole")
+            nc.vector.tensor_scalar(
+                out=whole[:], in0=angle[:], scalar1=ROUND_MAGIC, scalar2=ROUND_MAGIC,
+                op0=ALU.add, op1=ALU.subtract,
+            )
+            nc.vector.tensor_tensor(out=angle[:], in0=angle[:], in1=whole[:], op=ALU.subtract)
+
+        def table_waves(first_tile):
+            t = slice(first_tile, first_tile + ROUND)
+            nc.scalar.activation(out=cosine[:, t], in_=angle[:, t], func=ACT.Sin, scale=math.pi)
+            nc.scalar.activation(out=sine[:, t], in_=angle[:, t], func=ACT.Sin, scale=2.0 * math.pi)
+            nc.scalar.activation(out=cosine[:, t], in_=cosine[:, t], func=ACT.Square)
+            nc.scalar.activation(
+                out=cosine[:, t], in_=cosine[:, t], func=ACT.Copy, scale=-2.0, bias=1.0
+            )
+
+        def table_products(first_tile):
+            t = slice(first_tile, first_tile + ROUND)
+            shape = [P, ROUND, 2, PAIRS]
+            nc.vector.tensor_tensor(
+                out=cos_tab[:, t], in0=cosine[:, t].unsqueeze(2).to_broadcast(shape),
+                in1=zoom[:, t], op=ALU.mult,
+            )
+            nc.vector.tensor_tensor(
+                out=sin_tab[:, t], in0=sine[:, t].unsqueeze(2).to_broadcast(shape),
+                in1=zoom[:, t], op=ALU.mult,
+            )
+
+        def rotate(qk, t, rotated):
+            y = qk[:].rearrange("p (mj e) -> p mj e", e=2)
+            cos_t = cos_tab[:, t].rearrange("p m j -> p (m j)")
+            sin_t = sin_tab[:, t].rearrange("p m j -> p (m j)")
+            straight = work.tile([P, 2 * PAIRS, 2], F32, name="straight")
+            nc.vector.tensor_tensor(
+                out=straight[:], in0=y, in1=cos_t.unsqueeze(2).to_broadcast([P, 2 * PAIRS, 2]),
+                op=ALU.mult,
+            )
+            crossed = work.tile([P, 2, 2 * PAIRS], F32, name="crossed")
+            nc.vector.scalar_tensor_tensor(
+                out=crossed[:, 0, :], in0=y[:, :, 1], scalar=-1.0, in1=sin_t,
+                op0=ALU.mult, op1=ALU.mult,
+            )
+            nc.vector.tensor_tensor(out=crossed[:, 1, :], in0=y[:, :, 0], in1=sin_t, op=ALU.mult)
+            nc.gpsimd.tensor_tensor(
+                out=rotated.rearrange("p m (j e) -> p m j e", e=2),
+                in0=straight[:].rearrange("p (m j) e -> p m j e", m=2),
+                in1=crossed[:].rearrange("p e (m j) -> p m j e", m=2),
+                op=ALU.add,
+            )
+
+        def store(out, r, tile_rows):
+            rows = out[batch_of(r)].rearrange("(p t) d -> p (t d)", t=TILES)
+            first = first_tile_of(r) * DH
+            nc.sync.dma_start(out=rows[:, first : first + ROUND * DH], in_=tile_rows)
+
+        ident = const.tile([P, P], F32, name="ident")
+        make_identity(nc, ident[:])
+
+        x_raw = {}
+        wq_raw = load_w(w_q, "wq_raw")
+        x_raw[0] = load_x(0)
+        wk_raw = load_w(w_k, "wk_raw")
+        x_raw[1] = load_x(1)
+        wv_raw = load_w(w_v, "wv_raw")
+        for r in range(2, AHEAD):
+            x_raw[r] = load_x(r)
+
+        log_base, centred, pos_turns, freq = table_columns()
+        table_zoom(log_base, centred)
+        table_turns(pos_turns, freq)
+
+        x_mx = {}
+        x_grouped = transpose_x(x_raw[0])
+        wq_grouped = regroup_w(wq_raw)
+        table_fraction()
+        wq_mx = quantise_w(wq_grouped, "wq")
+        wk_grouped = regroup_w(wk_raw)
+        x_mx[0] = quantise_x(x_grouped)
+        wk_mx = quantise_w(wk_grouped, "wk")
+        wv_grouped = regroup_w(wv_raw)
+        table_waves(0)
+        table_products(0)
+        wv_mx = quantise_w(wv_grouped, "wv")
+
+        for r in range(ROUNDS):
+            if r + 1 < ROUNDS:
+                x_grouped = transpose_x(x_raw[r + 1])
+            if r + AHEAD < ROUNDS:
+                x_raw[r + AHEAD] = load_x(r + AHEAD)
+
+            qk_banks = []
+            for i in range(ROUND):
+                qk = qk_psum.tile([P, 2 * DH], F32, name="qk")
+                project(qk[:, 0:DH], x_mx[r], i, wq_mx)
+                project(qk[:, DH : 2 * DH], x_mx[r], i, wk_mx)
+                qk_banks.append(qk)
+            v_bank = v_psum.tile([P, ROUND, DH], F32, name="v_bank")
+            for i in range(ROUND):
+                project(v_bank[:, i, :], x_mx[r], i, wv_mx)
+
+            if r + 1 < ROUNDS:
+                x_mx[r + 1] = quantise_x(x_grouped)
+
+            next_tiles = first_tile_of(r) + ROUND
+            make_tables = batch_of(r) == 0 and next_tiles < TILES
+            if make_tables:
+                table_waves(next_tiles)
+
+            rotated = work.tile([P, 2, ROUND, DH], F32, name="rotated")
+            for i in range(ROUND):
+                rotate(qk_banks[i], first_tile_of(r) + i, rotated[:, :, i, :])
+            if make_tables:
+                table_products(next_tiles)
+            v_rows = work.tile([P, ROUND * DH], F32, name="v_rows")
+            nc.scalar.copy(out=v_rows[:], in_=v_bank[:].rearrange("p i d -> p (i d)"))
+
+            store(out_2, r, v_rows[:])
+            store(out_0, r, rotated[:, 0].rearrange("p i d -> p (i d)"))
+            store(out_1, r, rotated[:, 1].rearrange("p i d -> p (i d)"))

@@ -36,11 +36,11 @@ def tile_retblock_pa_kernel(tc, x, w_q, w_k, w_v, out_0, out_1, out_2):
     with ExitStack() as ctx:
         const = ctx.enter_context(tc.tile_pool(name="const", bufs=1))
         x_raw_pool = ctx.enter_context(tc.tile_pool(name="x_raw_pool", bufs=AHEAD))
-        x_mx_pool = ctx.enter_context(tc.tile_pool(name="x_mx_pool", bufs=3))
+        x_mx_pool = ctx.enter_context(tc.tile_pool(name="x_mx_pool", bufs=4))
         w_grouped_pool = ctx.enter_context(tc.tile_pool(name="w_grouped_pool", bufs=2))
         work = ctx.enter_context(tc.tile_pool(name="work", bufs=3))
-        xt_psum = ctx.enter_context(tc.psum_pool(name="xt_psum", bufs=4))
-        qk_psum = ctx.enter_context(tc.psum_pool(name="qk_psum", bufs=3))
+        xt_psum = ctx.enter_context(tc.psum_pool(name="xt_psum", bufs=3))
+        qk_psum = ctx.enter_context(tc.psum_pool(name="qk_psum", bufs=4))
         v_psum = ctx.enter_context(tc.psum_pool(name="v_psum", bufs=1))
         ctx.enter_context(tc.manual_schedule())
 
@@ -50,49 +50,57 @@ def tile_retblock_pa_kernel(tc, x, w_q, w_k, w_v, out_0, out_1, out_2):
         def first_tile_of(r):
             return (r // BATCH) * ROUND
 
-        def load_x(r):
+        def load_x(r, pieces=1):
             x_raw = x_raw_pool.tile([P, ROUND * HID], BF16, name="x_raw")
             rows = x[batch_of(r)].rearrange("(p t) k -> p (t k)", t=TILES)
             first = first_tile_of(r) * HID
-            nc.sync.dma_start(out=x_raw[:], in_=rows[:, first : first + ROUND * HID])
+            width = ROUND * HID // pieces
+            for c in range(0, ROUND * HID, width):
+                nc.sync.dma_start(
+                    out=x_raw[:, c : c + width], in_=rows[:, first + c : first + c + width]
+                )
             return x_raw
 
         def load_w(w, name):
             w_raw = const.tile([P, PASSES * PACK, DH], BF16, name=name)
-            nc.sync.dma_start(
-                out=w_raw[:].rearrange("p (g t) c -> p g (t c)", t=PACK),
-                in_=w.rearrange("(g p t) c -> p g (t c)", p=P, t=PACK),
-            )
+            for g in range(0, PASSES, 2):
+                nc.sync.dma_start(
+                    out=w_raw[:, g * PACK : (g + 2) * PACK].rearrange("p (g t) c -> p g (t c)", t=PACK),
+                    in_=w.rearrange("(g p t) c -> p g (t c)", p=P, t=PACK)[:, g : g + 2],
+                )
             return w_raw
 
-        def regroup_w(w_raw):
-            w_grouped = w_grouped_pool.tile(
+        def grouped_w():
+            return w_grouped_pool.tile(
                 [P, PASSES, DH, PACK], BF16, align_bytes=64, name="w_grouped"
             )
-            for g in range(PASSES):
-                nc.vector.tensor_copy(
-                    out=w_grouped[:, g].rearrange("p (c i) t -> p c t i", i=4),
-                    in_=w_raw[:, g * PACK : (g + 1) * PACK, :].rearrange(
-                        "p t (c i) -> p c t i", i=4
-                    ),
-                )
-            return w_grouped
 
-        def quantise_w(w_grouped, name):
+        def regroup_w(copy, w_grouped, w_raw, g):
+            copy(
+                out=w_grouped[:, g].rearrange("p (c i) t -> p c t i", i=4),
+                in_=w_raw[:, g * PACK : (g + 1) * PACK, :].rearrange(
+                    "p t (c i) -> p c t i", i=4
+                ),
+            )
+
+        def mx_w(name):
             codes = const.tile([P, PASSES * DH], U32, align_bytes=64, name=name + "_codes")
             scales = const.tile([P, PASSES * DH], U8, align_bytes=64, name=name + "_scales")
-            nc.vector.quantize_mx(
-                out=codes[:].bitcast(FP8X4),
-                scales=scales[:],
-                in_=w_grouped[:].rearrange("p g c t -> p (g c t)"),
-            )
             return codes, scales
 
-        def transpose_x(x_raw):
+        def quantise_w(w_mx, w_grouped, g):
+            codes, scales = w_mx
+            cols = slice(g * DH, (g + 2) * DH)
+            nc.vector.quantize_mx(
+                out=codes[:, cols].bitcast(FP8X4),
+                scales=scales[:, cols],
+                in_=w_grouped[:, g : g + 2].rearrange("p g c t -> p (g c t)"),
+            )
+
+        def transpose_x(x_raw, x_grouped, i):
             words = x_raw[:].bitcast(F32)
-            x_grouped = x_mx_pool.tile([P, ROUND * HID], BF16, align_bytes=64, name="x_grouped")
             grouped_words = x_grouped[:].bitcast(F32)
-            for bank in range(ROUND * WORDS // (4 * P)):
+            for bank in range(i * WORDS // (4 * P), (i + 1) * WORDS // (4 * P)):
                 xt = xt_psum.tile([P, 4, P], F32, name="xt")
                 for a in range(4):
                     start = (bank * 2 + a // 2) * 2 * P
@@ -106,22 +114,24 @@ def tile_retblock_pa_kernel(tc, x, w_q, w_k, w_v, out_0, out_1, out_2):
                     ),
                     in_=xt[:].rearrange("p (g u) r -> p g r u", u=2),
                 )
-            return x_grouped
 
-        def quantise_x(x_grouped):
+        def new_x():
+            x_grouped = x_mx_pool.tile([P, ROUND * HID], BF16, align_bytes=64, name="x_grouped")
             codes = x_mx_pool.tile([P, ROUND * PASSES * P], U32, align_bytes=64, name="x_codes")
             scales = x_mx_pool.tile([P, ROUND * PASSES * P], U8, align_bytes=64, name="x_scales")
-            for i in range(ROUND):
-                cols = slice(i * PASSES * P, (i + 1) * PASSES * P)
-                nc.vector.quantize_mx(
-                    out=codes[:, cols].bitcast(FP8X4),
-                    scales=scales[:, cols],
-                    in_=x_grouped[:, i * HID : (i + 1) * HID],
-                )
-            return codes, scales
+            return x_grouped, codes, scales
+
+        def quantise_x(x_parts, i):
+            x_grouped, codes, scales = x_parts
+            cols = slice(i * PASSES * P, (i + 1) * PASSES * P)
+            nc.vector.quantize_mx(
+                out=codes[:, cols].bitcast(FP8X4),
+                scales=scales[:, cols],
+                in_=x_grouped[:, i * HID : (i + 1) * HID],
+            )
 
         def project(out, x_mx, i, w_mx):
-            x_codes, x_scales = x_mx
+            x_grouped, x_codes, x_scales = x_mx
             w_codes, w_scales = w_mx
             for g in range(PASSES):
                 tokens = slice((i * PASSES + g) * P, (i * PASSES + g + 1) * P)
@@ -139,9 +149,10 @@ def tile_retblock_pa_kernel(tc, x, w_q, w_k, w_v, out_0, out_1, out_2):
         plain = [P, TILES, PAIRS]
         both = [P, TILES, 2, PAIRS]
         angle = const.tile(plain, F32, name="angle")
+        whole = const.tile(plain, F32, name="whole")
         zoom = const.tile(both, F32, name="zoom")
         sine = const.tile(plain, F32, name="sine")
-        cosine = const.tile(plain, F32, name="cosine")
+        versine = const.tile(plain, F32, name="versine")
         cos_tab = const.tile(both, F32, name="cos_tab")
         sin_tab = const.tile(both, F32, name="sin_tab")
 
@@ -159,11 +170,12 @@ def tile_retblock_pa_kernel(tc, x, w_q, w_k, w_v, out_0, out_1, out_2):
             nc.scalar.activation(out=log_base[:], in_=log_base[:], func=ACT.Ln)
             pos = const.tile([P, TILES], F32, name="pos")
             nc.vector.tensor_copy(out=pos[:], in_=pos_int[:])
-            centred = const.tile([P, TILES], F32, name="centred")
-            nc.vector.tensor_scalar(
-                out=centred[:], in0=pos[:], scalar1=float(SEQ // 2), scalar2=1.0 / SCALE_BASE,
-                op0=ALU.subtract, op1=ALU.mult,
-            )
+            centred = const.tile([P, 2, TILES], F32, name="centred")
+            for m, unit in ((0, 1.0 / SCALE_BASE), (1, -1.0 / SCALE_BASE)):
+                nc.vector.tensor_scalar(
+                    out=centred[:, m], in0=pos[:], scalar1=float(SEQ // 2), scalar2=unit,
+                    op0=ALU.subtract, op1=ALU.mult,
+                )
             pos_turns = const.tile([P, TILES], F32, name="pos_turns")
             nc.vector.tensor_scalar(
                 out=pos_turns[:], in0=pos[:], scalar1=1.0 / (2.0 * math.pi), scalar2=None,
@@ -180,54 +192,54 @@ def tile_retblock_pa_kernel(tc, x, w_q, w_k, w_v, out_0, out_1, out_2):
             return log_base, centred, pos_turns, freq
 
         def table_zoom(log_base, centred):
-            log_z = const.tile(plain, F32, name="log_z")
-            nc.vector.tensor_tensor(
-                out=log_z[:],
-                in0=centred[:].unsqueeze(2).to_broadcast(plain),
-                in1=log_base[:].unsqueeze(1).to_broadcast(plain),
-                op=ALU.mult,
-            )
-            nc.scalar.activation(out=zoom[:, :, 0, :], in_=log_z[:], func=ACT.Exp)
-            nc.scalar.activation(out=zoom[:, :, 1, :], in_=log_z[:], func=ACT.Exp, scale=-1.0)
+            for t in range(TILES):
+                nc.scalar.activation(
+                    out=zoom[:, t, 0, :], in_=log_base[:], func=ACT.Exp,
+                    scale=centred[:, 0, t : t + 1],
+                )
+                nc.scalar.activation(
+                    out=zoom[:, t, 1, :], in_=log_base[:], func=ACT.Exp,
+                    scale=centred[:, 1, t : t + 1],
+                )
 
-        def table_turns(pos_turns, freq):
-            nc.vector.tensor_tensor(
-                out=angle[:],
-                in0=pos_turns[:].unsqueeze(2).to_broadcast(plain),
-                in1=freq[:].unsqueeze(1).to_broadcast(plain),
-                op=ALU.mult,
-            )
+        def table_turns(pos_turns, freq, first_tile):
+            for t in range(first_tile, first_tile + ROUND):
+                nc.scalar.activation(
+                    out=angle[:, t], in_=freq[:], func=ACT.Copy, scale=pos_turns[:, t : t + 1]
+                )
 
-        def table_fraction():
-            whole = const.tile(plain, F32, name="whole")
+        def table_fraction(first_tile):
+            t = slice(first_tile, first_tile + ROUND)
             nc.vector.tensor_scalar(
-                out=whole[:], in0=angle[:], scalar1=ROUND_MAGIC, scalar2=ROUND_MAGIC,
+                out=whole[:, t], in0=angle[:, t], scalar1=ROUND_MAGIC, scalar2=ROUND_MAGIC,
                 op0=ALU.add, op1=ALU.subtract,
             )
-            nc.vector.tensor_tensor(out=angle[:], in0=angle[:], in1=whole[:], op=ALU.subtract)
+            nc.vector.tensor_tensor(
+                out=angle[:, t], in0=angle[:, t], in1=whole[:, t], op=ALU.subtract
+            )
 
         def table_waves(first_tile):
             t = slice(first_tile, first_tile + ROUND)
-            nc.scalar.activation(out=cosine[:, t], in_=angle[:, t], func=ACT.Sin, scale=math.pi)
+            nc.scalar.activation(out=versine[:, t], in_=angle[:, t], func=ACT.Sin, scale=math.pi)
             nc.scalar.activation(out=sine[:, t], in_=angle[:, t], func=ACT.Sin, scale=2.0 * math.pi)
-            nc.scalar.activation(out=cosine[:, t], in_=cosine[:, t], func=ACT.Square)
             nc.scalar.activation(
-                out=cosine[:, t], in_=cosine[:, t], func=ACT.Copy, scale=-2.0, bias=1.0
+                out=versine[:, t], in_=versine[:, t], func=ACT.Square, scale=math.sqrt(2.0)
             )
 
         def table_products(first_tile):
             t = slice(first_tile, first_tile + ROUND)
             shape = [P, ROUND, 2, PAIRS]
-            nc.vector.tensor_tensor(
-                out=cos_tab[:, t], in0=cosine[:, t].unsqueeze(2).to_broadcast(shape),
-                in1=zoom[:, t], op=ALU.mult,
-            )
+            for m in range(2):
+                nc.vector.scalar_tensor_tensor(
+                    out=cos_tab[:, t, m], in0=versine[:, t], scalar=1.0, in1=zoom[:, t, m],
+                    op0=ALU.subtract, op1=ALU.mult,
+                )
             nc.vector.tensor_tensor(
                 out=sin_tab[:, t], in0=sine[:, t].unsqueeze(2).to_broadcast(shape),
                 in1=zoom[:, t], op=ALU.mult,
             )
 
-        def rotate(qk, t, rotated):
+        def multiply(qk, t):
             y = qk[:].rearrange("p (mj e) -> p mj e", e=2)
             cos_t = cos_tab[:, t].rearrange("p m j -> p (m j)")
             sin_t = sin_tab[:, t].rearrange("p m j -> p (m j)")
@@ -242,11 +254,15 @@ def tile_retblock_pa_kernel(tc, x, w_q, w_k, w_v, out_0, out_1, out_2):
                 op0=ALU.mult, op1=ALU.mult,
             )
             nc.vector.tensor_tensor(out=crossed[:, 1, :], in0=y[:, :, 0], in1=sin_t, op=ALU.mult)
-            nc.gpsimd.tensor_tensor(
+            return straight, crossed
+
+        def combine(engine, products, rotated):
+            straight, crossed = products
+            engine.tensor_tensor(
                 out=rotated.rearrange("p m (j e) -> p m j e", e=2),
-                in0=straight[:].rearrange("p (m j) e -> p m j e", m=2),
-                in1=crossed[:].rearrange("p e (m j) -> p m j e", m=2),
-                op=ALU.add,
+                in0=crossed[:].rearrange("p e (m j) -> p m j e", m=2),
+                in1=straight[:].rearrange("p (m j) e -> p m j e", m=2),
+                op=ALU.subtract,
             )
 
         def store(out, r, tile_rows):
@@ -254,67 +270,140 @@ def tile_retblock_pa_kernel(tc, x, w_q, w_k, w_v, out_0, out_1, out_2):
             first = first_tile_of(r) * DH
             nc.sync.dma_start(out=rows[:, first : first + ROUND * DH], in_=tile_rows)
 
-        ident = const.tile([P, P], F32, name="ident")
-        make_identity(nc, ident[:])
+        def store_qk(r, rotated):
+            store(out_0, r, rotated[:, 0].rearrange("p i d -> p (i d)"))
+            store(out_1, r, rotated[:, 1].rearrange("p i d -> p (i d)"))
 
         x_raw = {}
         wq_raw = load_w(w_q, "wq_raw")
-        x_raw[0] = load_x(0)
+        x_raw[0] = load_x(0, pieces=ROUND)
         wk_raw = load_w(w_k, "wk_raw")
-        x_raw[1] = load_x(1)
+        x_raw[1] = load_x(1, pieces=ROUND)
         wv_raw = load_w(w_v, "wv_raw")
         for r in range(2, AHEAD):
             x_raw[r] = load_x(r)
 
         log_base, centred, pos_turns, freq = table_columns()
+        ident = const.tile([P, P], F32, name="ident")
+        make_identity(nc, ident[:])
         table_zoom(log_base, centred)
-        table_turns(pos_turns, freq)
+        for t in range(0, TILES, ROUND):
+            table_turns(pos_turns, freq, t)
 
         x_mx = {}
-        x_grouped = transpose_x(x_raw[0])
-        wq_grouped = regroup_w(wq_raw)
-        table_fraction()
-        wq_mx = quantise_w(wq_grouped, "wq")
-        wk_grouped = regroup_w(wk_raw)
-        x_mx[0] = quantise_x(x_grouped)
-        wk_mx = quantise_w(wk_grouped, "wk")
-        wv_grouped = regroup_w(wv_raw)
-        table_waves(0)
-        table_products(0)
-        wv_mx = quantise_w(wv_grouped, "wv")
+        qk_banks = {}
+        wq_mx, wk_mx, wv_mx = mx_w("wq"), mx_w("wk"), mx_w("wv")
 
-        for r in range(ROUNDS):
-            if r + 1 < ROUNDS:
-                x_grouped = transpose_x(x_raw[r + 1])
-            if r + AHEAD < ROUNDS:
-                x_raw[r + AHEAD] = load_x(r + AHEAD)
-
-            qk_banks = []
+        def transposes(r):
+            x_mx[r] = new_x()
             for i in range(ROUND):
-                qk = qk_psum.tile([P, 2 * DH], F32, name="qk")
-                project(qk[:, 0:DH], x_mx[r], i, wq_mx)
-                project(qk[:, DH : 2 * DH], x_mx[r], i, wk_mx)
-                qk_banks.append(qk)
+                transpose_x(x_raw[r], x_mx[r][0], i)
+
+        def project_q(r, i):
+            qk = qk_psum.tile([P, 2 * DH], F32, name="qk")
+            qk_banks[r, i] = qk
+            project(qk[:, 0:DH], x_mx[r], i, wq_mx)
+
+        def project_k(r, i):
+            project(qk_banks[r, i][:, DH : 2 * DH], x_mx[r], i, wk_mx)
+
+        def project_v(r):
             v_bank = v_psum.tile([P, ROUND, DH], F32, name="v_bank")
             for i in range(ROUND):
                 project(v_bank[:, i, :], x_mx[r], i, wv_mx)
-
-            if r + 1 < ROUNDS:
-                x_mx[r + 1] = quantise_x(x_grouped)
-
-            next_tiles = first_tile_of(r) + ROUND
-            make_tables = batch_of(r) == 0 and next_tiles < TILES
-            if make_tables:
-                table_waves(next_tiles)
-
-            rotated = work.tile([P, 2, ROUND, DH], F32, name="rotated")
-            for i in range(ROUND):
-                rotate(qk_banks[i], first_tile_of(r) + i, rotated[:, :, i, :])
-            if make_tables:
-                table_products(next_tiles)
             v_rows = work.tile([P, ROUND * DH], F32, name="v_rows")
             nc.scalar.copy(out=v_rows[:], in_=v_bank[:].rearrange("p i d -> p (i d)"))
-
             store(out_2, r, v_rows[:])
-            store(out_0, r, rotated[:, 0].rearrange("p i d -> p (i d)"))
-            store(out_1, r, rotated[:, 1].rearrange("p i d -> p (i d)"))
+
+        vector_copy, scalar_copy = nc.vector.tensor_copy, nc.scalar.copy
+        wq_grouped = grouped_w()
+        for g in range(PASSES):
+            regroup_w(vector_copy, wq_grouped, wq_raw, g)
+        quantise_w(wq_mx, wq_grouped, 0)
+        table_fraction(0)
+        quantise_w(wq_mx, wq_grouped, 2)
+
+        transposes(0)
+        wk_grouped = grouped_w()
+        quantise_x(x_mx[0], 0)
+        regroup_w(vector_copy, wk_grouped, wk_raw, 0)
+        regroup_w(vector_copy, wk_grouped, wk_raw, 1)
+        quantise_x(x_mx[0], 1)
+        for i in range(ROUND):
+            project_q(0, i)
+        regroup_w(scalar_copy, wk_grouped, wk_raw, 3)
+        quantise_w(wk_mx, wk_grouped, 0)
+        regroup_w(vector_copy, wk_grouped, wk_raw, 2)
+        table_waves(0)
+        quantise_w(wk_mx, wk_grouped, 2)
+        transposes(1)
+        for i in range(ROUND):
+            project_k(0, i)
+        quantise_x(x_mx[1], 0)
+        table_products(0)
+        quantise_x(x_mx[1], 1)
+        wv_grouped = grouped_w()
+        regroup_w(scalar_copy, wv_grouped, wv_raw, 0)
+        regroup_w(vector_copy, wv_grouped, wv_raw, 1)
+        regroup_w(vector_copy, wv_grouped, wv_raw, 2)
+        regroup_w(scalar_copy, wv_grouped, wv_raw, 3)
+        quantise_w(wv_mx, wv_grouped, 0)
+        quantise_w(wv_mx, wv_grouped, 2)
+
+        rotated = {}
+        products = {}
+
+        def multiplies(r, i):
+            if i == 0:
+                rotated[r] = work.tile([P, 2, ROUND, DH], F32, name="rotated")
+            products[r, i] = multiply(qk_banks[r, i], first_tile_of(r) + i)
+
+        def subtract(engine, r, i):
+            combine(engine, products[r, i], rotated[r][:, :, i, :])
+            if i == ROUND - 1:
+                store_qk(r, rotated[r])
+
+        project_q(1, 0)
+        project_k(1, 0)
+        multiplies(0, 0)
+        project_q(1, 1)
+        project_k(1, 1)
+        subtract(nc.gpsimd, 0, 0)
+        transposes(2)
+        multiplies(0, 1)
+        project_v(0)
+        quantise_x(x_mx[2], 0)
+        subtract(nc.vector, 0, 1)
+        quantise_x(x_mx[2], 1)
+        for t in range(ROUND, TILES, ROUND):
+            table_fraction(t)
+
+        for r in range(2, ROUNDS + 1):
+            if r - 2 + AHEAD < ROUNDS:
+                x_raw[r - 2 + AHEAD] = load_x(r - 2 + AHEAD)
+            next_tiles = first_tile_of(r - 1) + ROUND
+            make_tables = batch_of(r) == 0 and next_tiles < TILES
+            if r + 1 < ROUNDS:
+                transposes(r + 1)
+            if make_tables:
+                table_waves(next_tiles)
+            multiplies(r - 1, 0)
+            if r + 1 < ROUNDS:
+                quantise_x(x_mx[r + 1], 0)
+            subtract(nc.gpsimd, r - 1, 0)
+            multiplies(r - 1, 1)
+            if r + 1 < ROUNDS:
+                quantise_x(x_mx[r + 1], 1)
+            subtract(nc.vector, r - 1, 1)
+            if r == ROUNDS:
+                project_v(r - 1)
+            else:
+                if r == ROUNDS - 1:
+                    project_v(r - 1)
+                for i in range(ROUND):
+                    project_q(r, i)
+                    project_k(r, i)
+                if r < ROUNDS - 1:
+                    project_v(r - 1)
+            if make_tables:
+                table_products(next_tiles)

@@ -294,9 +294,10 @@ def tile_retblock_pa_kernel(tc, x, w_q, w_k, w_v, out_0, out_1, out_2):
         qk_banks = {}
         wq_mx, wk_mx, wv_mx = mx_w("wq"), mx_w("wk"), mx_w("wv")
 
-        def transposes(r):
-            x_mx[r] = new_x()
-            for i in range(ROUND):
+        def transposes(r, tiles=range(ROUND)):
+            if r not in x_mx:
+                x_mx[r] = new_x()
+            for i in tiles:
                 transpose_x(x_raw[r], x_mx[r][0], i)
 
         def project_q(r, i):
@@ -307,13 +308,16 @@ def tile_retblock_pa_kernel(tc, x, w_q, w_k, w_v, out_0, out_1, out_2):
         def project_k(r, i):
             project(qk_banks[r, i][:, DH : 2 * DH], x_mx[r], i, wk_mx)
 
-        def project_v(r):
-            v_bank = v_psum.tile([P, ROUND, DH], F32, name="v_bank")
-            for i in range(ROUND):
-                project(v_bank[:, i, :], x_mx[r], i, wv_mx)
-            v_rows = work.tile([P, ROUND * DH], F32, name="v_rows")
-            nc.scalar.copy(out=v_rows[:], in_=v_bank[:].rearrange("p i d -> p (i d)"))
-            store(out_2, r, v_rows[:])
+        v_banks = {}
+
+        def project_v(r, i):
+            if i == 0:
+                v_banks[r] = v_psum.tile([P, ROUND, DH], F32, name="v_bank")
+            project(v_banks[r][:, i, :], x_mx[r], i, wv_mx)
+            if i == ROUND - 1:
+                v_rows = work.tile([P, ROUND * DH], F32, name="v_rows")
+                nc.scalar.copy(out=v_rows[:], in_=v_banks[r][:].rearrange("p i d -> p (i d)"))
+                store(out_2, r, v_rows[:])
 
         vector_copy, scalar_copy = nc.vector.tensor_copy, nc.scalar.copy
         wq_grouped = grouped_w()
@@ -369,9 +373,11 @@ def tile_retblock_pa_kernel(tc, x, w_q, w_k, w_v, out_0, out_1, out_2):
         project_q(1, 1)
         project_k(1, 1)
         subtract(nc.gpsimd, 0, 0)
-        transposes(2)
+        transposes(2, [0])
+        project_v(0, 0)
+        transposes(2, [1])
         multiplies(0, 1)
-        project_v(0)
+        project_v(0, 1)
         quantise_x(x_mx[2], 0)
         subtract(nc.vector, 0, 1)
         quantise_x(x_mx[2], 1)
@@ -383,27 +389,18 @@ def tile_retblock_pa_kernel(tc, x, w_q, w_k, w_v, out_0, out_1, out_2):
                 x_raw[r - 2 + AHEAD] = load_x(r - 2 + AHEAD)
             next_tiles = first_tile_of(r - 1) + ROUND
             make_tables = batch_of(r) == 0 and next_tiles < TILES
-            if r + 1 < ROUNDS:
-                transposes(r + 1)
-            if make_tables:
-                table_waves(next_tiles)
-            multiplies(r - 1, 0)
-            if r + 1 < ROUNDS:
-                quantise_x(x_mx[r + 1], 0)
-            subtract(nc.gpsimd, r - 1, 0)
-            multiplies(r - 1, 1)
-            if r + 1 < ROUNDS:
-                quantise_x(x_mx[r + 1], 1)
-            subtract(nc.vector, r - 1, 1)
-            if r == ROUNDS:
-                project_v(r - 1)
-            else:
-                if r == ROUNDS - 1:
-                    project_v(r - 1)
-                for i in range(ROUND):
+            for i in range(ROUND):
+                if r + 1 < ROUNDS:
+                    transposes(r + 1, [i])
+                    if i == ROUND - 1 and make_tables:
+                        table_waves(next_tiles)
+                multiplies(r - 1, i)
+                if r + 1 < ROUNDS:
+                    quantise_x(x_mx[r + 1], i)
+                subtract(nc.gpsimd if i == 0 else nc.vector, r - 1, i)
+                if r < ROUNDS:
                     project_q(r, i)
                     project_k(r, i)
-                if r < ROUNDS - 1:
-                    project_v(r - 1)
+                project_v(r - 1, i)
             if make_tables:
                 table_products(next_tiles)

@@ -22,7 +22,9 @@ PASSES = HID // (P * PACK)
 WORDS = HID // 2
 ROUND = 2
 ROUNDS = BATCH * TILES // ROUND
-AHEAD = 5
+N_TILES = BATCH * TILES
+LAG = 4
+AHEAD = 8
 
 ROTARY_BASE = 10000.0
 SCALE_BASE = 512.0
@@ -36,9 +38,11 @@ def tile_retblock_pa_kernel(tc, x, w_q, w_k, w_v, out_0, out_1, out_2):
     with ExitStack() as ctx:
         const = ctx.enter_context(tc.tile_pool(name="const", bufs=1))
         x_raw_pool = ctx.enter_context(tc.tile_pool(name="x_raw_pool", bufs=AHEAD))
-        x_mx_pool = ctx.enter_context(tc.tile_pool(name="x_mx_pool", bufs=4))
+        x_grouped_pool = ctx.enter_context(tc.tile_pool(name="x_grouped_pool", bufs=3))
+        x_mx_pool = ctx.enter_context(tc.tile_pool(name="x_mx_pool", bufs=LAG // ROUND + 2))
         w_grouped_pool = ctx.enter_context(tc.tile_pool(name="w_grouped_pool", bufs=2))
         work = ctx.enter_context(tc.tile_pool(name="work", bufs=3))
+        v_pool = ctx.enter_context(tc.tile_pool(name="v_pool", bufs=5))
         xt_psum = ctx.enter_context(tc.psum_pool(name="xt_psum", bufs=3))
         qk_psum = ctx.enter_context(tc.psum_pool(name="qk_psum", bufs=4))
         v_psum = ctx.enter_context(tc.psum_pool(name="v_psum", bufs=1))
@@ -50,23 +54,22 @@ def tile_retblock_pa_kernel(tc, x, w_q, w_k, w_v, out_0, out_1, out_2):
         def first_tile_of(r):
             return (r // BATCH) * ROUND
 
-        def load_x(r, pieces=1):
-            x_raw = x_raw_pool.tile([P, ROUND * HID], BF16, name="x_raw")
-            rows = x[batch_of(r)].rearrange("(p t) k -> p (t k)", t=TILES)
-            first = first_tile_of(r) * HID
-            width = ROUND * HID // pieces
-            for c in range(0, ROUND * HID, width):
-                nc.sync.dma_start(
-                    out=x_raw[:, c : c + width], in_=rows[:, first + c : first + c + width]
-                )
-            return x_raw
+        def new_x_raw():
+            return x_raw_pool.tile([P, ROUND * HID], BF16, name="x_raw")
 
-        def load_w(w, name):
+        def load_x(x_raw, r, i, tiles=1):
+            rows = x[batch_of(r)].rearrange("(p t) k -> p (t k)", t=TILES)
+            first = (first_tile_of(r) + i) * HID
+            nc.sync.dma_start(
+                out=x_raw[:, i * HID : (i + tiles) * HID], in_=rows[:, first : first + tiles * HID]
+            )
+
+        def load_w(w, name, step=2):
             w_raw = const.tile([P, PASSES * PACK, DH], BF16, name=name)
-            for g in range(0, PASSES, 2):
+            for g in range(0, PASSES, step):
                 nc.sync.dma_start(
-                    out=w_raw[:, g * PACK : (g + 2) * PACK].rearrange("p (g t) c -> p g (t c)", t=PACK),
-                    in_=w.rearrange("(g p t) c -> p g (t c)", p=P, t=PACK)[:, g : g + 2],
+                    out=w_raw[:, g * PACK : (g + step) * PACK].rearrange("p (g t) c -> p g (t c)", t=PACK),
+                    in_=w.rearrange("(g p t) c -> p g (t c)", p=P, t=PACK)[:, g : g + step],
                 )
             return w_raw
 
@@ -116,7 +119,7 @@ def tile_retblock_pa_kernel(tc, x, w_q, w_k, w_v, out_0, out_1, out_2):
                 )
 
         def new_x():
-            x_grouped = x_mx_pool.tile([P, ROUND * HID], BF16, align_bytes=64, name="x_grouped")
+            x_grouped = x_grouped_pool.tile([P, ROUND * HID], BF16, align_bytes=64, name="x_grouped")
             codes = x_mx_pool.tile([P, ROUND * PASSES * P], U32, align_bytes=64, name="x_codes")
             scales = x_mx_pool.tile([P, ROUND * PASSES * P], U8, align_bytes=64, name="x_scales")
             return x_grouped, codes, scales
@@ -149,27 +152,28 @@ def tile_retblock_pa_kernel(tc, x, w_q, w_k, w_v, out_0, out_1, out_2):
         plain = [P, TILES, PAIRS]
         both = [P, TILES, 2, PAIRS]
         angle = const.tile(plain, F32, name="angle")
-        whole = const.tile(plain, F32, name="whole")
         zoom = const.tile(both, F32, name="zoom")
         sine = const.tile(plain, F32, name="sine")
         versine = const.tile(plain, F32, name="versine")
         cos_tab = const.tile(both, F32, name="cos_tab")
         sin_tab = const.tile(both, F32, name="sin_tab")
 
-        def table_columns():
-            j_int = const.tile([P, PAIRS], I32, name="j_int")
-            nc.gpsimd.iota(j_int[:], pattern=[[1, PAIRS]], base=0, channel_multiplier=0)
-            pos_int = const.tile([P, TILES], I32, name="pos_int")
-            nc.gpsimd.iota(pos_int[:], pattern=[[1, TILES]], base=0, channel_multiplier=TILES)
+        def table_columns(ident):
             log_base = const.tile([P, PAIRS], F32, name="log_base")
-            nc.vector.tensor_copy(out=log_base[:], in_=j_int[:])
+            nc.gpsimd.iota(
+                log_base[:], pattern=[[1, PAIRS]], base=0, channel_multiplier=0,
+                allow_small_or_imprecise_dtypes=True,
+            )
+            pos = const.tile([P, TILES], F32, name="pos")
+            nc.gpsimd.iota(
+                pos[:], pattern=[[1, TILES]], base=0, channel_multiplier=TILES,
+                allow_small_or_imprecise_dtypes=True,
+            )
             nc.vector.tensor_scalar(
                 out=log_base[:], in0=log_base[:], scalar1=2.0 / (1.4 * DH), scalar2=0.4 / 1.4,
                 op0=ALU.mult, op1=ALU.add,
             )
             nc.scalar.activation(out=log_base[:], in_=log_base[:], func=ACT.Ln)
-            pos = const.tile([P, TILES], F32, name="pos")
-            nc.vector.tensor_copy(out=pos[:], in_=pos_int[:])
             centred = const.tile([P, 2, TILES], F32, name="centred")
             for m, unit in ((0, 1.0 / SCALE_BASE), (1, -1.0 / SCALE_BASE)):
                 nc.vector.tensor_scalar(
@@ -182,10 +186,11 @@ def tile_retblock_pa_kernel(tc, x, w_q, w_k, w_v, out_0, out_1, out_2):
                 op0=ALU.mult,
             )
             freq = const.tile([P, PAIRS], F32, name="freq")
-            nc.vector.memset(freq[:, 0:1], 1.0)
+            make_identity(nc, ident[:])
+            nc.gpsimd.memset(freq[:, 0:1], 1.0)
             for doubling in range(7):
                 width = 2**doubling
-                nc.vector.tensor_scalar(
+                nc.gpsimd.tensor_scalar(
                     out=freq[:, width : 2 * width], in0=freq[:, 0:width],
                     scalar1=ROTARY_BASE ** (-width / PAIRS), scalar2=None, op0=ALU.mult,
                 )
@@ -204,18 +209,19 @@ def tile_retblock_pa_kernel(tc, x, w_q, w_k, w_v, out_0, out_1, out_2):
 
         def table_turns(pos_turns, freq, first_tile):
             for t in range(first_tile, first_tile + ROUND):
-                nc.scalar.activation(
-                    out=angle[:, t], in_=freq[:], func=ACT.Copy, scale=pos_turns[:, t : t + 1]
+                nc.vector.tensor_scalar(
+                    out=angle[:, t], in0=freq[:], scalar1=pos_turns[:, t : t + 1], scalar2=None,
+                    op0=ALU.mult,
                 )
 
         def table_fraction(first_tile):
             t = slice(first_tile, first_tile + ROUND)
             nc.vector.tensor_scalar(
-                out=whole[:, t], in0=angle[:, t], scalar1=ROUND_MAGIC, scalar2=ROUND_MAGIC,
+                out=versine[:, t], in0=angle[:, t], scalar1=ROUND_MAGIC, scalar2=ROUND_MAGIC,
                 op0=ALU.add, op1=ALU.subtract,
             )
             nc.vector.tensor_tensor(
-                out=angle[:, t], in0=angle[:, t], in1=whole[:, t], op=ALU.subtract
+                out=angle[:, t], in0=angle[:, t], in1=versine[:, t], op=ALU.subtract
             )
 
         def table_waves(first_tile):
@@ -265,142 +271,159 @@ def tile_retblock_pa_kernel(tc, x, w_q, w_k, w_v, out_0, out_1, out_2):
                 op=ALU.subtract,
             )
 
-        def store(out, r, tile_rows):
+        def store(out, r, i, tile_rows):
             rows = out[batch_of(r)].rearrange("(p t) d -> p (t d)", t=TILES)
-            first = first_tile_of(r) * DH
-            nc.sync.dma_start(out=rows[:, first : first + ROUND * DH], in_=tile_rows)
+            first = (first_tile_of(r) + i) * DH
+            nc.sync.dma_start(out=rows[:, first : first + tile_rows.shape[1]], in_=tile_rows)
 
-        def store_qk(r, rotated):
-            store(out_0, r, rotated[:, 0].rearrange("p i d -> p (i d)"))
-            store(out_1, r, rotated[:, 1].rearrange("p i d -> p (i d)"))
+        def store_qk(r, rotated, i, tiles):
+            for m, out in ((0, out_0), (1, out_1)):
+                store(out, r, i, rotated[:, m, i : i + tiles].rearrange("p i d -> p (i d)"))
 
-        x_raw = {}
-        wq_raw = load_w(w_q, "wq_raw")
-        x_raw[0] = load_x(0, pieces=ROUND)
+        x_raw = {0: new_x_raw()}
+        load_x(x_raw[0], 0, 0)
+        wq_raw = load_w(w_q, "wq_raw", step=1)
+        load_x(x_raw[0], 0, 1)
         wk_raw = load_w(w_k, "wk_raw")
-        x_raw[1] = load_x(1, pieces=ROUND)
+        x_raw[1] = new_x_raw()
+        for i in range(ROUND):
+            load_x(x_raw[1], 1, i)
         wv_raw = load_w(w_v, "wv_raw")
         for r in range(2, AHEAD):
-            x_raw[r] = load_x(r)
+            x_raw[r] = new_x_raw()
+            load_x(x_raw[r], r, 0, ROUND)
 
-        log_base, centred, pos_turns, freq = table_columns()
         ident = const.tile([P, P], F32, name="ident")
-        make_identity(nc, ident[:])
+        log_base, centred, pos_turns, freq = table_columns(ident)
         table_zoom(log_base, centred)
-        for t in range(0, TILES, ROUND):
-            table_turns(pos_turns, freq, t)
+        table_turns(pos_turns, freq, 0)
 
         x_mx = {}
         qk_banks = {}
-        wq_mx, wk_mx, wv_mx = mx_w("wq"), mx_w("wk"), mx_w("wv")
-
-        def transposes(r, tiles=range(ROUND)):
-            if r not in x_mx:
-                x_mx[r] = new_x()
-            for i in tiles:
-                transpose_x(x_raw[r], x_mx[r][0], i)
-
-        def project_q(r, i):
-            qk = qk_psum.tile([P, 2 * DH], F32, name="qk")
-            qk_banks[r, i] = qk
-            project(qk[:, 0:DH], x_mx[r], i, wq_mx)
-
-        def project_k(r, i):
-            project(qk_banks[r, i][:, DH : 2 * DH], x_mx[r], i, wk_mx)
-
         v_banks = {}
-
-        def project_v(r, i):
-            if i == 0:
-                v_banks[r] = v_psum.tile([P, ROUND, DH], F32, name="v_bank")
-            project(v_banks[r][:, i, :], x_mx[r], i, wv_mx)
-            if i == ROUND - 1:
-                v_rows = work.tile([P, ROUND * DH], F32, name="v_rows")
-                nc.scalar.copy(out=v_rows[:], in_=v_banks[r][:].rearrange("p i d -> p (i d)"))
-                store(out_2, r, v_rows[:])
-
+        rotated = {}
+        products = {}
+        wq_mx, wk_mx, wv_mx = mx_w("wq"), mx_w("wk"), mx_w("wv")
+        wq_grouped, wk_grouped = grouped_w(), grouped_w()
         vector_copy, scalar_copy = nc.vector.tensor_copy, nc.scalar.copy
-        wq_grouped = grouped_w()
-        for g in range(PASSES):
-            regroup_w(vector_copy, wq_grouped, wq_raw, g)
-        quantise_w(wq_mx, wq_grouped, 0)
-        table_fraction(0)
-        quantise_w(wq_mx, wq_grouped, 2)
+
+        def transposes(n):
+            r, i = divmod(n, ROUND)
+            if i == 0:
+                x_mx[r] = new_x()
+            transpose_x(x_raw[r], x_mx[r][0], i)
+
+        def quantise(n):
+            quantise_x(x_mx[n // ROUND], n % ROUND)
+
+        def project_q(n):
+            qk = qk_psum.tile([P, 2 * DH], F32, name="qk")
+            qk_banks[n] = qk
+            project(qk[:, 0:DH], x_mx[n // ROUND], n % ROUND, wq_mx)
+
+        def project_k(n):
+            project(qk_banks[n][:, DH : 2 * DH], x_mx[n // ROUND], n % ROUND, wk_mx)
+
+        def project_v(n):
+            r, i = divmod(n, ROUND)
+            if i == 0 and n < N_TILES - LAG:
+                v_tile = v_psum.tile([P, ROUND * DH], F32, name="v_bank")
+                v_banks[r] = v_tile[:]
+            elif i == 0 or r == ROUNDS - 1:
+                v_tile = xt_psum.tile([P, 4, P], F32, name="xt")
+                v_banks[r] = v_tile[:].rearrange("p a r -> p (a r)")
+            project(v_banks[r][:, i * DH : (i + 1) * DH], x_mx[r], i, wv_mx)
+            if r == ROUNDS - 1:
+                v_rows = v_pool.tile([P, ROUND * DH], F32, name="v_rows")
+                nc.scalar.copy(out=v_rows[:, 0:DH], in_=v_banks[r][:, i * DH : (i + 1) * DH])
+                store(out_2, r, i, v_rows[:, 0:DH])
+            elif i == ROUND - 1:
+                v_rows = v_pool.tile([P, ROUND * DH], F32, name="v_rows")
+                nc.scalar.copy(out=v_rows[:], in_=v_banks[r])
+                store(out_2, r, 0, v_rows[:])
+
+        def multiplies(n):
+            r, i = divmod(n, ROUND)
+            if i == 0:
+                rotated[r] = work.tile([P, 2, ROUND, DH], F32, name="rotated")
+            products[n] = multiply(qk_banks[n], first_tile_of(r) + i)
+
+        def subtract(engine, n):
+            r, i = divmod(n, ROUND)
+            combine(engine, products[n], rotated[r][:, :, i, :])
+            if r == ROUNDS - 1:
+                store_qk(r, rotated[r], i, 1)
+            elif i == ROUND - 1:
+                store_qk(r, rotated[r], 0, ROUND)
 
         transposes(0)
-        wk_grouped = grouped_w()
-        quantise_x(x_mx[0], 0)
-        regroup_w(vector_copy, wk_grouped, wk_raw, 0)
-        regroup_w(vector_copy, wk_grouped, wk_raw, 1)
-        quantise_x(x_mx[0], 1)
-        for i in range(ROUND):
-            project_q(0, i)
-        regroup_w(scalar_copy, wk_grouped, wk_raw, 3)
-        quantise_w(wk_mx, wk_grouped, 0)
-        regroup_w(vector_copy, wk_grouped, wk_raw, 2)
-        table_waves(0)
-        quantise_w(wk_mx, wk_grouped, 2)
+        for g in range(PASSES - 1):
+            regroup_w(vector_copy, wq_grouped, wq_raw, g)
+        regroup_w(scalar_copy, wq_grouped, wq_raw, PASSES - 1)
+        quantise_w(wq_mx, wq_grouped, 0)
+        quantise(0)
+        quantise_w(wq_mx, wq_grouped, 2)
+        table_fraction(0)
         transposes(1)
-        for i in range(ROUND):
-            project_k(0, i)
-        quantise_x(x_mx[1], 0)
+        project_q(0)
+        table_waves(0)
+        regroup_w(vector_copy, wk_grouped, wk_raw, 0)
+        quantise(1)
+        for g in range(1, PASSES):
+            regroup_w(vector_copy, wk_grouped, wk_raw, g)
+        quantise_w(wk_mx, wk_grouped, 0)
+        quantise_w(wk_mx, wk_grouped, 2)
+        transposes(2)
+        project_q(1)
+        quantise(2)
+        transposes(3)
+        project_k(0)
+        project_k(1)
         table_products(0)
-        quantise_x(x_mx[1], 1)
+        quantise(3)
+        project_q(2)
+        project_k(2)
+        multiplies(0)
         wv_grouped = grouped_w()
         regroup_w(scalar_copy, wv_grouped, wv_raw, 0)
-        regroup_w(vector_copy, wv_grouped, wv_raw, 1)
-        regroup_w(vector_copy, wv_grouped, wv_raw, 2)
+        regroup_w(scalar_copy, wv_grouped, wv_raw, 1)
+        subtract(nc.gpsimd, 0)
+        transposes(4)
+        multiplies(1)
+        regroup_w(scalar_copy, wv_grouped, wv_raw, 2)
         regroup_w(scalar_copy, wv_grouped, wv_raw, 3)
+        quantise(4)
+        table_turns(pos_turns, freq, ROUND)
+        table_fraction(ROUND)
+        subtract(nc.gpsimd, 1)
         quantise_w(wv_mx, wv_grouped, 0)
         quantise_w(wv_mx, wv_grouped, 2)
 
-        rotated = {}
-        products = {}
-
-        def multiplies(r, i):
-            if i == 0:
-                rotated[r] = work.tile([P, 2, ROUND, DH], F32, name="rotated")
-            products[r, i] = multiply(qk_banks[r, i], first_tile_of(r) + i)
-
-        def subtract(engine, r, i):
-            combine(engine, products[r, i], rotated[r][:, :, i, :])
-            if i == ROUND - 1:
-                store_qk(r, rotated[r])
-
-        project_q(1, 0)
-        project_k(1, 0)
-        multiplies(0, 0)
-        project_q(1, 1)
-        project_k(1, 1)
-        subtract(nc.gpsimd, 0, 0)
-        transposes(2, [0])
-        project_v(0, 0)
-        transposes(2, [1])
-        multiplies(0, 1)
-        project_v(0, 1)
-        quantise_x(x_mx[2], 0)
-        subtract(nc.vector, 0, 1)
-        quantise_x(x_mx[2], 1)
-        for t in range(ROUND, TILES, ROUND):
-            table_fraction(t)
-
-        for r in range(2, ROUNDS + 1):
-            if r - 2 + AHEAD < ROUNDS:
-                x_raw[r - 2 + AHEAD] = load_x(r - 2 + AHEAD)
-            next_tiles = first_tile_of(r - 1) + ROUND
-            make_tables = batch_of(r) == 0 and next_tiles < TILES
-            for i in range(ROUND):
-                if r + 1 < ROUNDS:
-                    transposes(r + 1, [i])
-                    if i == ROUND - 1 and make_tables:
-                        table_waves(next_tiles)
-                multiplies(r - 1, i)
-                if r + 1 < ROUNDS:
-                    quantise_x(x_mx[r + 1], i)
-                subtract(nc.gpsimd if i == 0 else nc.vector, r - 1, i)
-                if r < ROUNDS:
-                    project_q(r, i)
-                    project_k(r, i)
-                project_v(r - 1, i)
-            if make_tables:
-                table_products(next_tiles)
+        for n in range(3, N_TILES + 1):
+            r, i = divmod(n, ROUND)
+            new_tables = n % (2 * ROUND) == 0 and n < N_TILES
+            if n + 2 < N_TILES:
+                transposes(n + 2)
+                if n == 3:
+                    table_waves(ROUND)
+                elif n % (2 * ROUND) == 1 and first_tile_of(r) + ROUND < TILES:
+                    table_waves(first_tile_of(r) + ROUND)
+            if n - 1 >= 2:
+                multiplies(n - 1)
+            if n + 2 < N_TILES:
+                quantise(n + 2)
+            if new_tables:
+                table_products(first_tile_of(r))
+            if n - 1 >= 2:
+                subtract(nc.gpsimd if (n - 1) % ROUND == 0 else (nc.gpsimd if n < N_TILES else nc.vector), n - 1)
+            if new_tables and first_tile_of(r) + ROUND < TILES:
+                table_turns(pos_turns, freq, first_tile_of(r) + ROUND)
+                table_fraction(first_tile_of(r) + ROUND)
+            if n < N_TILES:
+                project_q(n)
+                project_k(n)
+            if LAG <= n < N_TILES:
+                project_v(n - LAG)
+            if n == N_TILES:
+                for late in range(N_TILES - LAG, N_TILES):
+                    project_v(late)

@@ -344,7 +344,7 @@ def tile_retblock_pa_kernel(tc, x, w_q, w_k, w_v, out_0, out_1, out_2):
 
         def multiplies(n):
             r, i = divmod(n, ROUND)
-            if i == 0:
+            if i == 0 or r == ROUNDS - 1:
                 rotated[r] = work.tile([P, 2, ROUND, DH], F32, name="rotated")
             products[n] = multiply(qk_banks[n], first_tile_of(r) + i)
 
@@ -395,7 +395,7 @@ def tile_retblock_pa_kernel(tc, x, w_q, w_k, w_v, out_0, out_1, out_2):
         quantise(4)
         table_turns(pos_turns, freq, ROUND)
         table_fraction(ROUND)
-        subtract(nc.gpsimd, 1)
+        subtract(nc.vector, 1)
         quantise_w(wv_mx, wv_grouped, 0)
         quantise_w(wv_mx, wv_grouped, 2)
 
@@ -415,7 +415,7 @@ def tile_retblock_pa_kernel(tc, x, w_q, w_k, w_v, out_0, out_1, out_2):
             if new_tables:
                 table_products(first_tile_of(r))
             if n - 1 >= 2:
-                subtract(nc.gpsimd if (n - 1) % ROUND == 0 else (nc.gpsimd if n < N_TILES else nc.vector), n - 1)
+                subtract(nc.gpsimd if (n - 1) % ROUND == 0 else nc.vector, n - 1)
             if new_tables and first_tile_of(r) + ROUND < TILES:
                 table_turns(pos_turns, freq, first_tile_of(r) + ROUND)
                 table_fraction(first_tile_of(r) + ROUND)

@@ -169,31 +169,36 @@ def tile_retblock_pa_kernel(tc, x, w_q, w_k, w_v, out_0, out_1, out_2):
                 pos[:], pattern=[[1, TILES]], base=0, channel_multiplier=TILES,
                 allow_small_or_imprecise_dtypes=True,
             )
+            make_identity(nc, ident[:])
+            centred = const.tile([P, 2, TILES], F32, name="centred")
+            pos_turns = const.tile([P, TILES], F32, name="pos_turns")
+            freq = const.tile([P, PAIRS], F32, name="freq")
+
+            def double(width):
+                nc.vector.tensor_scalar(
+                    out=freq[:, width : 2 * width], in0=freq[:, 0:width],
+                    scalar1=ROTARY_BASE ** (-width / PAIRS), scalar2=None, op0=ALU.mult,
+                )
+
+            nc.vector.memset(freq[:, 0:1], 1.0)
             nc.vector.tensor_scalar(
                 out=log_base[:], in0=log_base[:], scalar1=2.0 / (1.4 * DH), scalar2=0.4 / 1.4,
                 op0=ALU.mult, op1=ALU.add,
             )
             nc.scalar.activation(out=log_base[:], in_=log_base[:], func=ACT.Ln)
-            centred = const.tile([P, 2, TILES], F32, name="centred")
+            double(1)
             for m, unit in ((0, 1.0 / SCALE_BASE), (1, -1.0 / SCALE_BASE)):
                 nc.vector.tensor_scalar(
                     out=centred[:, m], in0=pos[:], scalar1=float(SEQ // 2), scalar2=unit,
                     op0=ALU.subtract, op1=ALU.mult,
                 )
-            pos_turns = const.tile([P, TILES], F32, name="pos_turns")
+                double(2 ** (m + 1))
             nc.vector.tensor_scalar(
                 out=pos_turns[:], in0=pos[:], scalar1=1.0 / (2.0 * math.pi), scalar2=None,
                 op0=ALU.mult,
             )
-            freq = const.tile([P, PAIRS], F32, name="freq")
-            make_identity(nc, ident[:])
-            nc.gpsimd.memset(freq[:, 0:1], 1.0)
-            for doubling in range(7):
-                width = 2**doubling
-                nc.gpsimd.tensor_scalar(
-                    out=freq[:, width : 2 * width], in0=freq[:, 0:width],
-                    scalar1=ROTARY_BASE ** (-width / PAIRS), scalar2=None, op0=ALU.mult,
-                )
+            for doubling in range(3, 7):
+                double(2**doubling)
             return log_base, centred, pos_turns, freq
 
         def table_zoom(log_base, centred):
@@ -207,22 +212,22 @@ def tile_retblock_pa_kernel(tc, x, w_q, w_k, w_v, out_0, out_1, out_2):
                     scale=centred[:, 1, t : t + 1],
                 )
 
-        def table_turns(pos_turns, freq, first_tile):
-            for t in range(first_tile, first_tile + ROUND):
+        def table_turns(pos_turns, freq):
+            halves = (slice(0, TILES // 2), slice(TILES // 2, TILES))
+            for t in range(TILES):
                 nc.vector.tensor_scalar(
                     out=angle[:, t], in0=freq[:], scalar1=pos_turns[:, t : t + 1], scalar2=None,
                     op0=ALU.mult,
                 )
-
-        def table_fraction(first_tile):
-            t = slice(first_tile, first_tile + ROUND)
-            nc.vector.tensor_scalar(
-                out=versine[:, t], in0=angle[:, t], scalar1=ROUND_MAGIC, scalar2=ROUND_MAGIC,
-                op0=ALU.add, op1=ALU.subtract,
-            )
-            nc.vector.tensor_tensor(
-                out=angle[:, t], in0=angle[:, t], in1=versine[:, t], op=ALU.subtract
-            )
+            for t in halves:
+                nc.vector.tensor_scalar(
+                    out=versine[:, t], in0=angle[:, t], scalar1=ROUND_MAGIC, scalar2=ROUND_MAGIC,
+                    op0=ALU.add, op1=ALU.subtract,
+                )
+            for t in halves:
+                nc.vector.tensor_tensor(
+                    out=angle[:, t], in0=angle[:, t], in1=versine[:, t], op=ALU.subtract
+                )
 
         def table_waves(first_tile):
             t = slice(first_tile, first_tile + ROUND)
@@ -296,7 +301,7 @@ def tile_retblock_pa_kernel(tc, x, w_q, w_k, w_v, out_0, out_1, out_2):
         ident = const.tile([P, P], F32, name="ident")
         log_base, centred, pos_turns, freq = table_columns(ident)
         table_zoom(log_base, centred)
-        table_turns(pos_turns, freq, 0)
+        table_turns(pos_turns, freq)
 
         x_mx = {}
         qk_banks = {}
@@ -363,7 +368,6 @@ def tile_retblock_pa_kernel(tc, x, w_q, w_k, w_v, out_0, out_1, out_2):
         quantise_w(wq_mx, wq_grouped, 0)
         quantise(0)
         quantise_w(wq_mx, wq_grouped, 2)
-        table_fraction(0)
         transposes(1)
         project_q(0)
         table_waves(0)
@@ -387,14 +391,12 @@ def tile_retblock_pa_kernel(tc, x, w_q, w_k, w_v, out_0, out_1, out_2):
         wv_grouped = grouped_w()
         regroup_w(scalar_copy, wv_grouped, wv_raw, 0)
         regroup_w(scalar_copy, wv_grouped, wv_raw, 1)
-        subtract(nc.gpsimd, 0)
         transposes(4)
         multiplies(1)
+        subtract(nc.gpsimd, 0)
         regroup_w(scalar_copy, wv_grouped, wv_raw, 2)
         regroup_w(scalar_copy, wv_grouped, wv_raw, 3)
         quantise(4)
-        table_turns(pos_turns, freq, ROUND)
-        table_fraction(ROUND)
         subtract(nc.vector, 1)
         quantise_w(wv_mx, wv_grouped, 0)
         quantise_w(wv_mx, wv_grouped, 2)
@@ -408,17 +410,16 @@ def tile_retblock_pa_kernel(tc, x, w_q, w_k, w_v, out_0, out_1, out_2):
                     table_waves(ROUND)
                 elif n % (2 * ROUND) == 1 and first_tile_of(r) + ROUND < TILES:
                     table_waves(first_tile_of(r) + ROUND)
-            if n - 1 >= 2:
+            if i == 0 and n - 1 >= 3 or n == N_TILES:
+                multiplies(n - 2)
                 multiplies(n - 1)
+                subtract(nc.gpsimd, n - 2)
             if n + 2 < N_TILES:
                 quantise(n + 2)
             if new_tables:
                 table_products(first_tile_of(r))
-            if n - 1 >= 2:
-                subtract(nc.gpsimd if (n - 1) % ROUND == 0 else nc.vector, n - 1)
-            if new_tables and first_tile_of(r) + ROUND < TILES:
-                table_turns(pos_turns, freq, first_tile_of(r) + ROUND)
-                table_fraction(first_tile_of(r) + ROUND)
+            if i == 0 and n - 1 >= 3 or n == N_TILES:
+                subtract(nc.vector, n - 1)
             if n < N_TILES:
                 project_q(n)
                 project_k(n)

@@ -38,7 +38,8 @@ def tile_retblock_pa_kernel(tc, x, w_q, w_k, w_v, out_0, out_1, out_2):
     with ExitStack() as ctx:
         const = ctx.enter_context(tc.tile_pool(name="const", bufs=1))
         x_raw_pool = ctx.enter_context(tc.tile_pool(name="x_raw_pool", bufs=AHEAD))
-        x_grouped_pool = ctx.enter_context(tc.tile_pool(name="x_grouped_pool", bufs=3))
+        x_words_pool = ctx.enter_context(tc.tile_pool(name="x_words_pool", bufs=2))
+        x_grouped_pool = ctx.enter_context(tc.tile_pool(name="x_grouped_pool", bufs=4))
         x_mx_pool = ctx.enter_context(tc.tile_pool(name="x_mx_pool", bufs=LAG // ROUND + 2))
         w_grouped_pool = ctx.enter_context(tc.tile_pool(name="w_grouped_pool", bufs=2))
         work = ctx.enter_context(tc.tile_pool(name="work", bufs=3))
@@ -100,16 +101,29 @@ def tile_retblock_pa_kernel(tc, x, w_q, w_k, w_v, out_0, out_1, out_2):
                 in_=w_grouped[:, g : g + 2].rearrange("p g c t -> p (g c t)"),
             )
 
-        def transpose_x(x_raw, x_grouped, i):
+        def permute_x(copy, x_raw, i):
+            x_words = x_words_pool.tile([P, WORDS], F32, align_bytes=64, name="x_words")
+            copy(
+                out=x_words[:].rearrange("p (g u w) -> p g u w", g=PASSES, u=2),
+                in_=x_raw[:].bitcast(F32)[:, i * WORDS : (i + 1) * WORDS].rearrange(
+                    "p (g w u) -> p g u w", g=PASSES, u=2
+                ),
+            )
+            return x_words
+
+        def transpose_x(x_raw, x_words, x_grouped, i):
             words = x_raw[:].bitcast(F32)
             grouped_words = x_grouped[:].bitcast(F32)
-            for bank in range(i * WORDS // (4 * P), (i + 1) * WORDS // (4 * P)):
+            for bank in range(WORDS // (4 * P)):
                 xt = xt_psum.tile([P, 4, P], F32, name="xt")
                 for a in range(4):
-                    start = (bank * 2 + a // 2) * 2 * P
-                    nc.tensor.transpose(
-                        xt[:, a, :], words[:, start + a % 2 : start + 2 * P : 2], ident[:]
-                    )
+                    if x_words is None:
+                        start = i * WORDS + (bank * 2 + a // 2) * 2 * P
+                        column = words[:, start + a % 2 : start + 2 * P : 2]
+                    else:
+                        start = (bank * 4 + a) * P
+                        column = x_words[:, start : start + P]
+                    nc.tensor.transpose(xt[:, a, :], column, ident[:])
                 first = bank * 4 * P
                 nc.scalar.copy(
                     out=grouped_words[:, first : first + 4 * P].rearrange(
@@ -119,22 +133,21 @@ def tile_retblock_pa_kernel(tc, x, w_q, w_k, w_v, out_0, out_1, out_2):
                 )
 
         def new_x():
-            x_grouped = x_grouped_pool.tile([P, ROUND * HID], BF16, align_bytes=64, name="x_grouped")
             codes = x_mx_pool.tile([P, ROUND * PASSES * P], U32, align_bytes=64, name="x_codes")
             scales = x_mx_pool.tile([P, ROUND * PASSES * P], U8, align_bytes=64, name="x_scales")
-            return x_grouped, codes, scales
+            return codes, scales
 
-        def quantise_x(x_parts, i):
-            x_grouped, codes, scales = x_parts
+        def quantise_x(x_grouped, x_parts, i):
+            codes, scales = x_parts
             cols = slice(i * PASSES * P, (i + 1) * PASSES * P)
             nc.vector.quantize_mx(
                 out=codes[:, cols].bitcast(FP8X4),
                 scales=scales[:, cols],
-                in_=x_grouped[:, i * HID : (i + 1) * HID],
+                in_=x_grouped[:],
             )
 
         def project(out, x_mx, i, w_mx):
-            x_grouped, x_codes, x_scales = x_mx
+            x_codes, x_scales = x_mx
             w_codes, w_scales = w_mx
             for g in range(PASSES):
                 tokens = slice((i * PASSES + g) * P, (i * PASSES + g + 1) * P)
@@ -306,6 +319,8 @@ def tile_retblock_pa_kernel(tc, x, w_q, w_k, w_v, out_0, out_1, out_2):
         x_mx = {}
         qk_banks = {}
         v_banks = {}
+        x_grouped = {}
+        x_words = {}
         rotated = {}
         products = {}
         wq_mx, wk_mx, wv_mx = mx_w("wq"), mx_w("wk"), mx_w("wv")
@@ -316,10 +331,11 @@ def tile_retblock_pa_kernel(tc, x, w_q, w_k, w_v, out_0, out_1, out_2):
             r, i = divmod(n, ROUND)
             if i == 0:
                 x_mx[r] = new_x()
-            transpose_x(x_raw[r], x_mx[r][0], i)
+            x_grouped[n] = x_grouped_pool.tile([P, HID], BF16, align_bytes=64, name="x_grouped")
+            transpose_x(x_raw[r], x_words.get(n), x_grouped[n], i)
 
         def quantise(n):
-            quantise_x(x_mx[n // ROUND], n % ROUND)
+            quantise_x(x_grouped[n], x_mx[n // ROUND], n % ROUND)
 
         def project_q(n):
             qk = qk_psum.tile([P, 2 * DH], F32, name="qk")
@@ -349,12 +365,12 @@ def tile_retblock_pa_kernel(tc, x, w_q, w_k, w_v, out_0, out_1, out_2):
 
         def multiplies(n):
             r, i = divmod(n, ROUND)
-            if i == 0 or r == ROUNDS - 1:
-                rotated[r] = work.tile([P, 2, ROUND, DH], F32, name="rotated")
             products[n] = multiply(qk_banks[n], first_tile_of(r) + i)
 
         def subtract(engine, n):
             r, i = divmod(n, ROUND)
+            if i == 0 or r == ROUNDS - 1:
+                rotated[r] = work.tile([P, 2, ROUND, DH], F32, name="rotated")
             combine(engine, products[n], rotated[r][:, :, i, :])
             if r == ROUNDS - 1:
                 store_qk(r, rotated[r], i, 1)
@@ -410,6 +426,8 @@ def tile_retblock_pa_kernel(tc, x, w_q, w_k, w_v, out_0, out_1, out_2):
                     table_waves(ROUND)
                 elif n % (2 * ROUND) == 1 and first_tile_of(r) + ROUND < TILES:
                     table_waves(first_tile_of(r) + ROUND)
+            if 4 <= n and n + 4 < N_TILES and n % 2 == 0:
+                x_words[n + 4] = permute_x(scalar_copy, x_raw[(n + 4) // ROUND], (n + 4) % ROUND)
             if i == 0 and n - 1 >= 3 or n == N_TILES:
                 multiplies(n - 2)
                 multiplies(n - 1)

@@ -28,6 +28,7 @@ AHEAD = 8
 
 ROTARY_BASE = 10000.0
 SCALE_BASE = 512.0
+FAST = math.ceil(PAIRS * math.log((SEQ - 1) / math.pi) / math.log(ROTARY_BASE))
 ROUND_MAGIC = 1.5 * 2.0**23
 
 FLOPS = 2 * BATCH * SEQ * HID * 3 * DH
@@ -227,6 +228,7 @@ def tile_retblock_pa_kernel(tc, x, w_q, w_k, w_v, out_0, out_1, out_2):
 
         def table_turns(pos_turns, freq):
             halves = (slice(0, TILES // 2), slice(TILES // 2, TILES))
+            whole = versine[:, :, 0:FAST]
             for t in range(TILES):
                 nc.vector.tensor_scalar(
                     out=angle[:, t], in0=freq[:], scalar1=pos_turns[:, t : t + 1], scalar2=None,
@@ -234,12 +236,13 @@ def tile_retblock_pa_kernel(tc, x, w_q, w_k, w_v, out_0, out_1, out_2):
                 )
             for t in halves:
                 nc.vector.tensor_scalar(
-                    out=versine[:, t], in0=angle[:, t], scalar1=ROUND_MAGIC, scalar2=ROUND_MAGIC,
-                    op0=ALU.add, op1=ALU.subtract,
+                    out=whole[:, t], in0=angle[:, t, 0:FAST], scalar1=ROUND_MAGIC,
+                    scalar2=ROUND_MAGIC, op0=ALU.add, op1=ALU.subtract,
                 )
             for t in halves:
                 nc.vector.tensor_tensor(
-                    out=angle[:, t], in0=angle[:, t], in1=versine[:, t], op=ALU.subtract
+                    out=angle[:, t, 0:FAST], in0=angle[:, t, 0:FAST], in1=whole[:, t],
+                    op=ALU.subtract,
                 )
 
         def table_waves(first_tile):
@@ -420,6 +423,9 @@ def tile_retblock_pa_kernel(tc, x, w_q, w_k, w_v, out_0, out_1, out_2):
         for n in range(3, N_TILES + 1):
             r, i = divmod(n, ROUND)
             new_tables = n % (2 * ROUND) == 0 and n < N_TILES
+            if n == N_TILES:
+                for late in range(N_TILES - LAG, N_TILES):
+                    project_v(late)
             if n + 2 < N_TILES:
                 transposes(n + 2)
                 if n == 3:
@@ -443,6 +449,3 @@ def tile_retblock_pa_kernel(tc, x, w_q, w_k, w_v, out_0, out_1, out_2):
                 project_k(n)
             if LAG <= n < N_TILES:
                 project_v(n - LAG)
-            if n == N_TILES:
-                for late in range(N_TILES - LAG, N_TILES):
-                    project_v(late)

@@ -412,7 +412,7 @@ def tile_retblock_pa_kernel(tc, x, w_q, w_k, w_v, out_0, out_1, out_2):
         regroup_w(scalar_copy, wv_grouped, wv_raw, 1)
         transposes(4)
         multiplies(1)
-        subtract(nc.gpsimd, 0)
+        subtract(nc.vector, 0)
         regroup_w(scalar_copy, wv_grouped, wv_raw, 2)
         regroup_w(scalar_copy, wv_grouped, wv_raw, 3)
         quantise(4)
@@ -437,7 +437,7 @@ def tile_retblock_pa_kernel(tc, x, w_q, w_k, w_v, out_0, out_1, out_2):
             if i == 0 and n - 1 >= 3 or n == N_TILES:
                 multiplies(n - 2)
                 multiplies(n - 1)
-                subtract(nc.gpsimd, n - 2)
+                subtract(nc.vector, n - 2)
             if n + 2 < N_TILES:
                 quantise(n + 2)
             if new_tables:

@@ -337,6 +337,14 @@ def tile_retblock_pa_kernel(tc, x, w_q, w_k, w_v, out_0, out_1, out_2):
             x_grouped[n] = x_grouped_pool.tile([P, HID], BF16, align_bytes=64, name="x_grouped")
             transpose_x(x_raw[r], x_words.get(n), x_grouped[n], i)
 
+        idle = const.tile([P, ROUND * DH], BF16, name="idle")
+        nc.gpsimd.memset(idle[:], 0.0)
+
+        def keep_warm(count):
+            bank = v_psum.tile([P, ROUND * DH], F32, name="v_bank")
+            for repeat in range(count):
+                nc.tensor.matmul(bank[:], lhsT=idle[:, 0:P], rhs=idle[:], start=True, stop=True)
+
         def quantise(n):
             quantise_x(x_grouped[n], x_mx[n // ROUND], n % ROUND)
 
@@ -380,7 +388,9 @@ def tile_retblock_pa_kernel(tc, x, w_q, w_k, w_v, out_0, out_1, out_2):
             elif i == ROUND - 1:
                 store_qk(r, rotated[r], 0, ROUND)
 
+        keep_warm(4)
         transposes(0)
+        keep_warm(6)
         for g in range(PASSES - 1):
             regroup_w(vector_copy, wq_grouped, wq_raw, g)
         regroup_w(scalar_copy, wq_grouped, wq_raw, PASSES - 1)
@@ -388,7 +398,9 @@ def tile_retblock_pa_kernel(tc, x, w_q, w_k, w_v, out_0, out_1, out_2):
         quantise(0)
         quantise_w(wq_mx, wq_grouped, 2)
         transposes(1)
+        keep_warm(1)
         project_q(0)
+        keep_warm(3)
         table_waves(0)
         regroup_w(vector_copy, wk_grouped, wk_raw, 0)
         quantise(1)
@@ -432,7 +444,7 @@ def tile_retblock_pa_kernel(tc, x, w_q, w_k, w_v, out_0, out_1, out_2):
                     table_waves(ROUND)
                 elif n % (2 * ROUND) == 1 and first_tile_of(r) + ROUND < TILES:
                     table_waves(first_tile_of(r) + ROUND)
-            if 4 <= n and n + 4 < N_TILES and n % 2 == 0:
+            if 4 <= n and n + 4 < N_TILES and n % 3 != 0:
                 x_words[n + 4] = permute_x(scalar_copy, x_raw[(n + 4) // ROUND], (n + 4) % ROUND)
             if i == 0 and n - 1 >= 3 or n == N_TILES:
                 multiplies(n - 2)

@@ -337,14 +337,6 @@ def tile_retblock_pa_kernel(tc, x, w_q, w_k, w_v, out_0, out_1, out_2):
             x_grouped[n] = x_grouped_pool.tile([P, HID], BF16, align_bytes=64, name="x_grouped")
             transpose_x(x_raw[r], x_words.get(n), x_grouped[n], i)
 
-        idle = const.tile([P, ROUND * DH], BF16, name="idle")
-        nc.gpsimd.memset(idle[:], 0.0)
-
-        def keep_warm(count):
-            bank = v_psum.tile([P, ROUND * DH], F32, name="v_bank")
-            for repeat in range(count):
-                nc.tensor.matmul(bank[:], lhsT=idle[:, 0:P], rhs=idle[:], start=True, stop=True)
-
         def quantise(n):
             quantise_x(x_grouped[n], x_mx[n // ROUND], n % ROUND)
 
@@ -388,9 +380,7 @@ def tile_retblock_pa_kernel(tc, x, w_q, w_k, w_v, out_0, out_1, out_2):
             elif i == ROUND - 1:
                 store_qk(r, rotated[r], 0, ROUND)
 
-        keep_warm(4)
         transposes(0)
-        keep_warm(6)
         for g in range(PASSES - 1):
             regroup_w(vector_copy, wq_grouped, wq_raw, g)
         regroup_w(scalar_copy, wq_grouped, wq_raw, PASSES - 1)
@@ -398,9 +388,7 @@ def tile_retblock_pa_kernel(tc, x, w_q, w_k, w_v, out_0, out_1, out_2):
         quantise(0)
         quantise_w(wq_mx, wq_grouped, 2)
         transposes(1)
-        keep_warm(1)
         project_q(0)
-        keep_warm(3)
         table_waves(0)
         regroup_w(vector_copy, wk_grouped, wk_raw, 0)
         quantise(1)
@@ -424,20 +412,20 @@ def tile_retblock_pa_kernel(tc, x, w_q, w_k, w_v, out_0, out_1, out_2):
         regroup_w(scalar_copy, wv_grouped, wv_raw, 1)
         transposes(4)
         multiplies(1)
-        subtract(nc.vector, 0)
+        subtract(nc.gpsimd, 0)
         regroup_w(scalar_copy, wv_grouped, wv_raw, 2)
-        regroup_w(scalar_copy, wv_grouped, wv_raw, 3)
         quantise(4)
+        regroup_w(vector_copy, wv_grouped, wv_raw, 3)
         subtract(nc.vector, 1)
         quantise_w(wv_mx, wv_grouped, 0)
         quantise_w(wv_mx, wv_grouped, 2)
 
         for n in range(3, N_TILES + 1):
             r, i = divmod(n, ROUND)
-            new_tables = n % (2 * ROUND) == 0 and n < N_TILES
             if n == N_TILES:
                 for late in range(N_TILES - LAG, N_TILES):
                     project_v(late)
+            new_tables = n % (2 * ROUND) == 0 and n < N_TILES
             if n + 2 < N_TILES:
                 transposes(n + 2)
                 if n == 3:
@@ -449,7 +437,7 @@ def tile_retblock_pa_kernel(tc, x, w_q, w_k, w_v, out_0, out_1, out_2):
             if i == 0 and n - 1 >= 3 or n == N_TILES:
                 multiplies(n - 2)
                 multiplies(n - 1)
-                subtract(nc.vector, n - 2)
+                subtract(nc.gpsimd, n - 2)
             if n + 2 < N_TILES:
                 quantise(n + 2)
             if new_tables:

@@ -6,7 +6,6 @@ from concourse.masks import make_identity
 
 F32 = mybir.dt.float32
 BF16 = mybir.dt.bfloat16
-I32 = mybir.dt.int32
 U32 = mybir.dt.uint32
 U8 = mybir.dt.uint8
 FP8X4 = mybir.dt.float8_e4m3fn_x4
@@ -17,14 +16,14 @@ P = 128
 BATCH, SEQ, HID, DH = 2, 1024, 2048, 256
 PAIRS = DH // 2
 TILES = SEQ // P
+ALL_TILES = BATCH * TILES
 PACK = 4
 PASSES = HID // (P * PACK)
 WORDS = HID // 2
 ROUND = 2
-ROUNDS = BATCH * TILES // ROUND
-N_TILES = BATCH * TILES
+ROUNDS = ALL_TILES // ROUND
+AHEAD = 2
 LAG = 4
-AHEAD = 8
 
 ROTARY_BASE = 10000.0
 SCALE_BASE = 512.0
@@ -38,13 +37,13 @@ def tile_retblock_pa_kernel(tc, x, w_q, w_k, w_v, out_0, out_1, out_2):
     nc = tc.nc
     with ExitStack() as ctx:
         const = ctx.enter_context(tc.tile_pool(name="const", bufs=1))
-        x_raw_pool = ctx.enter_context(tc.tile_pool(name="x_raw_pool", bufs=AHEAD))
-        x_words_pool = ctx.enter_context(tc.tile_pool(name="x_words_pool", bufs=2))
+        x_raw_pool = ctx.enter_context(tc.tile_pool(name="x_raw_pool", bufs=ROUNDS))
+        x_sorted_pool = ctx.enter_context(tc.tile_pool(name="x_sorted_pool", bufs=2))
         x_grouped_pool = ctx.enter_context(tc.tile_pool(name="x_grouped_pool", bufs=4))
         x_mx_pool = ctx.enter_context(tc.tile_pool(name="x_mx_pool", bufs=LAG // ROUND + 2))
         w_grouped_pool = ctx.enter_context(tc.tile_pool(name="w_grouped_pool", bufs=2))
         work = ctx.enter_context(tc.tile_pool(name="work", bufs=3))
-        v_pool = ctx.enter_context(tc.tile_pool(name="v_pool", bufs=5))
+        v_rows_pool = ctx.enter_context(tc.tile_pool(name="v_rows_pool", bufs=5))
         xt_psum = ctx.enter_context(tc.psum_pool(name="xt_psum", bufs=3))
         qk_psum = ctx.enter_context(tc.psum_pool(name="qk_psum", bufs=4))
         v_psum = ctx.enter_context(tc.psum_pool(name="v_psum", bufs=1))
@@ -59,23 +58,25 @@ def tile_retblock_pa_kernel(tc, x, w_q, w_k, w_v, out_0, out_1, out_2):
         def new_x_raw():
             return x_raw_pool.tile([P, ROUND * HID], BF16, name="x_raw")
 
-        def load_x(x_raw, r, i, tiles=1):
+        def load_x(n, tiles=1):
+            r, i = divmod(n, ROUND)
             rows = x[batch_of(r)].rearrange("(p t) k -> p (t k)", t=TILES)
             first = (first_tile_of(r) + i) * HID
             nc.sync.dma_start(
-                out=x_raw[:, i * HID : (i + tiles) * HID], in_=rows[:, first : first + tiles * HID]
+                out=x_raw[r][:, i * HID : (i + tiles) * HID],
+                in_=rows[:, first : first + tiles * HID],
             )
 
-        def load_w(w, name, step=2):
-            w_raw = const.tile([P, PASSES * PACK, DH], BF16, name=name)
-            for g in range(0, PASSES, step):
-                nc.sync.dma_start(
-                    out=w_raw[:, g * PACK : (g + step) * PACK].rearrange("p (g t) c -> p g (t c)", t=PACK),
-                    in_=w.rearrange("(g p t) c -> p g (t c)", p=P, t=PACK)[:, g : g + step],
-                )
-            return w_raw
+        def new_w_raw(name):
+            return const.tile([P, PASSES * PACK, DH], BF16, name=name)
 
-        def grouped_w():
+        def load_w(w, w_raw, first, end):
+            nc.sync.dma_start(
+                out=w_raw[:, first * PACK : end * PACK].rearrange("p (g t) c -> p g (t c)", t=PACK),
+                in_=w.rearrange("(g p t) c -> p g (t c)", p=P, t=PACK)[:, first:end],
+            )
+
+        def new_w_grouped():
             return w_grouped_pool.tile(
                 [P, PASSES, DH, PACK], BF16, align_bytes=64, name="w_grouped"
             )
@@ -88,7 +89,7 @@ def tile_retblock_pa_kernel(tc, x, w_q, w_k, w_v, out_0, out_1, out_2):
                 ),
             )
 
-        def mx_w(name):
+        def new_w_mx(name):
             codes = const.tile([P, PASSES * DH], U32, align_bytes=64, name=name + "_codes")
             scales = const.tile([P, PASSES * DH], U8, align_bytes=64, name=name + "_scales")
             return codes, scales
@@ -102,28 +103,31 @@ def tile_retblock_pa_kernel(tc, x, w_q, w_k, w_v, out_0, out_1, out_2):
                 in_=w_grouped[:, g : g + 2].rearrange("p g c t -> p (g c t)"),
             )
 
-        def permute_x(copy, x_raw, i):
-            x_words = x_words_pool.tile([P, WORDS], F32, align_bytes=64, name="x_words")
-            copy(
-                out=x_words[:].rearrange("p (g u w) -> p g u w", g=PASSES, u=2),
-                in_=x_raw[:].bitcast(F32)[:, i * WORDS : (i + 1) * WORDS].rearrange(
-                    "p (g w u) -> p g u w", g=PASSES, u=2
-                ),
-            )
-            return x_words
+        def words_of(n):
+            r, i = divmod(n, ROUND)
+            return x_raw[r][:].bitcast(F32)[:, i * WORDS : (i + 1) * WORDS]
 
-        def transpose_x(x_raw, x_words, x_grouped, i):
-            words = x_raw[:].bitcast(F32)
-            grouped_words = x_grouped[:].bitcast(F32)
+        def sort_words(n):
+            x_sorted[n] = x_sorted_pool.tile([P, WORDS], F32, align_bytes=64, name="x_sorted")
+            nc.scalar.copy(
+                out=x_sorted[n][:].rearrange("p (g u w) -> p g u w", g=PASSES, u=2),
+                in_=words_of(n).rearrange("p (g w u) -> p g u w", g=PASSES, u=2),
+            )
+
+        def transpose(n):
+            if n % ROUND == 0:
+                x_mx[n // ROUND] = new_x_mx()
+            x_grouped[n] = x_grouped_pool.tile([P, HID], BF16, align_bytes=64, name="x_grouped")
+            grouped_words = x_grouped[n][:].bitcast(F32)
             for bank in range(WORDS // (4 * P)):
                 xt = xt_psum.tile([P, 4, P], F32, name="xt")
                 for a in range(4):
-                    if x_words is None:
-                        start = i * WORDS + (bank * 2 + a // 2) * 2 * P
-                        column = words[:, start + a % 2 : start + 2 * P : 2]
+                    if n in x_sorted:
+                        first = (bank * 4 + a) * P
+                        column = x_sorted[n][:, first : first + P]
                     else:
-                        start = (bank * 4 + a) * P
-                        column = x_words[:, start : start + P]
+                        first = (bank * 2 + a // 2) * 2 * P
+                        column = words_of(n)[:, first + a % 2 : first + 2 * P : 2]
                     nc.tensor.transpose(xt[:, a, :], column, ident[:])
                 first = bank * 4 * P
                 nc.scalar.copy(
@@ -133,22 +137,22 @@ def tile_retblock_pa_kernel(tc, x, w_q, w_k, w_v, out_0, out_1, out_2):
                     in_=xt[:].rearrange("p (g u) r -> p g r u", u=2),
                 )
 
-        def new_x():
+        def new_x_mx():
             codes = x_mx_pool.tile([P, ROUND * PASSES * P], U32, align_bytes=64, name="x_codes")
             scales = x_mx_pool.tile([P, ROUND * PASSES * P], U8, align_bytes=64, name="x_scales")
             return codes, scales
 
-        def quantise_x(x_grouped, x_parts, i):
-            codes, scales = x_parts
+        def quantise_x(n):
+            r, i = divmod(n, ROUND)
+            codes, scales = x_mx[r]
             cols = slice(i * PASSES * P, (i + 1) * PASSES * P)
             nc.vector.quantize_mx(
-                out=codes[:, cols].bitcast(FP8X4),
-                scales=scales[:, cols],
-                in_=x_grouped[:],
+                out=codes[:, cols].bitcast(FP8X4), scales=scales[:, cols], in_=x_grouped[n][:]
             )
 
-        def project(out, x_mx, i, w_mx):
-            x_codes, x_scales = x_mx
+        def project(out, n, w_mx):
+            r, i = divmod(n, ROUND)
+            x_codes, x_scales = x_mx[r]
             w_codes, w_scales = w_mx
             for g in range(PASSES):
                 tokens = slice((i * PASSES + g) * P, (i * PASSES + g + 1) * P)
@@ -163,6 +167,33 @@ def tile_retblock_pa_kernel(tc, x, w_q, w_k, w_v, out_0, out_1, out_2):
                     stop=(g == PASSES - 1),
                 )
 
+        def project_q(n):
+            qk_banks[n] = qk_psum.tile([P, 2 * DH], F32, name="qk")
+            project(qk_banks[n][:, 0:DH], n, wq_mx)
+
+        def project_k(n):
+            project(qk_banks[n][:, DH : 2 * DH], n, wk_mx)
+
+        def project_v(n):
+            r, i = divmod(n, ROUND)
+            last = r == ROUNDS - 1
+            if i == 0 or last:
+                if n < ALL_TILES - LAG:
+                    v_banks[r] = v_psum.tile([P, ROUND * DH], F32, name="v_bank")[:]
+                else:
+                    v_banks[r] = xt_psum.tile([P, 4, P], F32, name="xt")[:].rearrange(
+                        "p a r -> p (a r)"
+                    )
+            project(v_banks[r][:, i * DH : (i + 1) * DH], n, wv_mx)
+            if last or i == ROUND - 1:
+                first = i if last else 0
+                width = (i + 1 - first) * DH
+                v_rows = v_rows_pool.tile([P, ROUND * DH], F32, name="v_rows")
+                nc.scalar.copy(
+                    out=v_rows[:, 0:width], in_=v_banks[r][:, first * DH : first * DH + width]
+                )
+                store(out_2, r, first, v_rows[:, 0:width])
+
         plain = [P, TILES, PAIRS]
         both = [P, TILES, 2, PAIRS]
         angle = const.tile(plain, F32, name="angle")
@@ -172,21 +203,13 @@ def tile_retblock_pa_kernel(tc, x, w_q, w_k, w_v, out_0, out_1, out_2):
         cos_tab = const.tile(both, F32, name="cos_tab")
         sin_tab = const.tile(both, F32, name="sin_tab")
 
-        def table_columns(ident):
-            log_base = const.tile([P, PAIRS], F32, name="log_base")
+        def table_columns():
+            iota_options = dict(base=0, allow_small_or_imprecise_dtypes=True)
             nc.gpsimd.iota(
-                log_base[:], pattern=[[1, PAIRS]], base=0, channel_multiplier=0,
-                allow_small_or_imprecise_dtypes=True,
+                log_base[:], pattern=[[1, PAIRS]], channel_multiplier=0, **iota_options
             )
-            pos = const.tile([P, TILES], F32, name="pos")
-            nc.gpsimd.iota(
-                pos[:], pattern=[[1, TILES]], base=0, channel_multiplier=TILES,
-                allow_small_or_imprecise_dtypes=True,
-            )
+            nc.gpsimd.iota(pos[:], pattern=[[1, TILES]], channel_multiplier=TILES, **iota_options)
             make_identity(nc, ident[:])
-            centred = const.tile([P, 2, TILES], F32, name="centred")
-            pos_turns = const.tile([P, TILES], F32, name="pos_turns")
-            freq = const.tile([P, PAIRS], F32, name="freq")
 
             def double(width):
                 nc.vector.tensor_scalar(
@@ -213,22 +236,18 @@ def tile_retblock_pa_kernel(tc, x, w_q, w_k, w_v, out_0, out_1, out_2):
             )
             for doubling in range(3, 7):
                 double(2**doubling)
-            return log_base, centred, pos_turns, freq
 
-        def table_zoom(log_base, centred):
+        def table_zoom():
             for t in range(TILES):
-                nc.scalar.activation(
-                    out=zoom[:, t, 0, :], in_=log_base[:], func=ACT.Exp,
-                    scale=centred[:, 0, t : t + 1],
-                )
-                nc.scalar.activation(
-                    out=zoom[:, t, 1, :], in_=log_base[:], func=ACT.Exp,
-                    scale=centred[:, 1, t : t + 1],
-                )
+                for m in range(2):
+                    nc.scalar.activation(
+                        out=zoom[:, t, m, :], in_=log_base[:], func=ACT.Exp,
+                        scale=centred[:, m, t : t + 1],
+                    )
 
-        def table_turns(pos_turns, freq):
+        def table_turns():
             halves = (slice(0, TILES // 2), slice(TILES // 2, TILES))
-            whole = versine[:, :, 0:FAST]
+            fast_angle, whole = angle[:, :, 0:FAST], versine[:, :, 0:FAST]
             for t in range(TILES):
                 nc.vector.tensor_scalar(
                     out=angle[:, t], in0=freq[:], scalar1=pos_turns[:, t : t + 1], scalar2=None,
@@ -236,13 +255,12 @@ def tile_retblock_pa_kernel(tc, x, w_q, w_k, w_v, out_0, out_1, out_2):
                 )
             for t in halves:
                 nc.vector.tensor_scalar(
-                    out=whole[:, t], in0=angle[:, t, 0:FAST], scalar1=ROUND_MAGIC,
+                    out=whole[:, t], in0=fast_angle[:, t], scalar1=ROUND_MAGIC,
                     scalar2=ROUND_MAGIC, op0=ALU.add, op1=ALU.subtract,
                 )
             for t in halves:
                 nc.vector.tensor_tensor(
-                    out=angle[:, t, 0:FAST], in0=angle[:, t, 0:FAST], in1=whole[:, t],
-                    op=ALU.subtract,
+                    out=fast_angle[:, t], in0=fast_angle[:, t], in1=whole[:, t], op=ALU.subtract
                 )
 
         def table_waves(first_tile):
@@ -255,19 +273,21 @@ def tile_retblock_pa_kernel(tc, x, w_q, w_k, w_v, out_0, out_1, out_2):
 
         def table_products(first_tile):
             t = slice(first_tile, first_tile + ROUND)
-            shape = [P, ROUND, 2, PAIRS]
             for m in range(2):
                 nc.vector.scalar_tensor_tensor(
                     out=cos_tab[:, t, m], in0=versine[:, t], scalar=1.0, in1=zoom[:, t, m],
                     op0=ALU.subtract, op1=ALU.mult,
                 )
             nc.vector.tensor_tensor(
-                out=sin_tab[:, t], in0=sine[:, t].unsqueeze(2).to_broadcast(shape),
+                out=sin_tab[:, t],
+                in0=sine[:, t].unsqueeze(2).to_broadcast([P, ROUND, 2, PAIRS]),
                 in1=zoom[:, t], op=ALU.mult,
             )
 
-        def multiply(qk, t):
-            y = qk[:].rearrange("p (mj e) -> p mj e", e=2)
+        def multiply(n):
+            r, i = divmod(n, ROUND)
+            t = first_tile_of(r) + i
+            y = qk_banks[n][:].rearrange("p (mj e) -> p mj e", e=2)
             cos_t = cos_tab[:, t].rearrange("p m j -> p (m j)")
             sin_t = sin_tab[:, t].rearrange("p m j -> p (m j)")
             straight = work.tile([P, 2 * PAIRS, 2], F32, name="straight")
@@ -281,171 +301,132 @@ def tile_retblock_pa_kernel(tc, x, w_q, w_k, w_v, out_0, out_1, out_2):
                 op0=ALU.mult, op1=ALU.mult,
             )
             nc.vector.tensor_tensor(out=crossed[:, 1, :], in0=y[:, :, 0], in1=sin_t, op=ALU.mult)
-            return straight, crossed
+            terms[n] = straight, crossed
 
-        def combine(engine, products, rotated):
-            straight, crossed = products
+        def subtract(engine, n):
+            r, i = divmod(n, ROUND)
+            last = r == ROUNDS - 1
+            if i == 0 or last:
+                rotated[r] = work.tile([P, 2, ROUND, DH], F32, name="rotated")
+            straight, crossed = terms[n]
             engine.tensor_tensor(
-                out=rotated.rearrange("p m (j e) -> p m j e", e=2),
+                out=rotated[r][:, :, i, :].rearrange("p m (j e) -> p m j e", e=2),
                 in0=crossed[:].rearrange("p e (m j) -> p m j e", m=2),
                 in1=straight[:].rearrange("p (m j) e -> p m j e", m=2),
                 op=ALU.subtract,
             )
+            if last or i == ROUND - 1:
+                first = i if last else 0
+                for m, out in ((0, out_0), (1, out_1)):
+                    rows = rotated[r][:, m, first : i + 1].rearrange("p i d -> p (i d)")
+                    store(out, r, first, rows)
 
         def store(out, r, i, tile_rows):
             rows = out[batch_of(r)].rearrange("(p t) d -> p (t d)", t=TILES)
             first = (first_tile_of(r) + i) * DH
             nc.sync.dma_start(out=rows[:, first : first + tile_rows.shape[1]], in_=tile_rows)
 
-        def store_qk(r, rotated, i, tiles):
-            for m, out in ((0, out_0), (1, out_1)):
-                store(out, r, i, rotated[:, m, i : i + tiles].rearrange("p i d -> p (i d)"))
+        x_raw, x_sorted, x_grouped, x_mx = {}, {}, {}, {}
+        qk_banks, v_banks, terms, rotated = {}, {}, {}, {}
+        for r in range(ROUNDS):
+            x_raw[r] = x_raw_pool.tile([P, ROUND * HID], BF16, name="x_raw")
+        wq_raw, wk_raw, wv_raw = new_w_raw("wq_raw"), new_w_raw("wk_raw"), new_w_raw("wv_raw")
 
-        x_raw = {0: new_x_raw()}
-        load_x(x_raw[0], 0, 0)
-        wq_raw = load_w(w_q, "wq_raw", step=1)
-        load_x(x_raw[0], 0, 1)
-        wk_raw = load_w(w_k, "wk_raw")
-        x_raw[1] = new_x_raw()
-        for i in range(ROUND):
-            load_x(x_raw[1], 1, i)
-        wv_raw = load_w(w_v, "wv_raw")
-        for r in range(2, AHEAD):
-            x_raw[r] = new_x_raw()
-            load_x(x_raw[r], r, 0, ROUND)
+        load_x(0)
+        for g in range(PASSES):
+            load_w(w_q, wq_raw, g, g + 1)
+        load_x(1)
+        load_w(w_k, wk_raw, 0, PASSES // 2)
+        load_x(2)
+        load_w(w_k, wk_raw, PASSES // 2, PASSES)
+        load_x(3)
+        load_w(w_v, wv_raw, 0, PASSES // 2)
+        load_w(w_v, wv_raw, PASSES // 2, PASSES)
+        load_x(4)
+        load_x(5)
+        for n in range(6, ALL_TILES, ROUND):
+            load_x(n, tiles=ROUND)
 
         ident = const.tile([P, P], F32, name="ident")
-        log_base, centred, pos_turns, freq = table_columns(ident)
-        table_zoom(log_base, centred)
-        table_turns(pos_turns, freq)
+        log_base = const.tile([P, PAIRS], F32, name="log_base")
+        pos = const.tile([P, TILES], F32, name="pos")
+        centred = const.tile([P, 2, TILES], F32, name="centred")
+        pos_turns = const.tile([P, TILES], F32, name="pos_turns")
+        freq = const.tile([P, PAIRS], F32, name="freq")
+        table_columns()
+        table_zoom()
+        table_turns()
 
-        x_mx = {}
-        qk_banks = {}
-        v_banks = {}
-        x_grouped = {}
-        x_words = {}
-        rotated = {}
-        products = {}
-        wq_mx, wk_mx, wv_mx = mx_w("wq"), mx_w("wk"), mx_w("wv")
-        wq_grouped, wk_grouped = grouped_w(), grouped_w()
+        wq_mx, wk_mx, wv_mx = new_w_mx("wq"), new_w_mx("wk"), new_w_mx("wv")
+        wq_grouped, wk_grouped = new_w_grouped(), new_w_grouped()
         vector_copy, scalar_copy = nc.vector.tensor_copy, nc.scalar.copy
 
-        def transposes(n):
-            r, i = divmod(n, ROUND)
-            if i == 0:
-                x_mx[r] = new_x()
-            x_grouped[n] = x_grouped_pool.tile([P, HID], BF16, align_bytes=64, name="x_grouped")
-            transpose_x(x_raw[r], x_words.get(n), x_grouped[n], i)
-
-        def quantise(n):
-            quantise_x(x_grouped[n], x_mx[n // ROUND], n % ROUND)
-
-        def project_q(n):
-            qk = qk_psum.tile([P, 2 * DH], F32, name="qk")
-            qk_banks[n] = qk
-            project(qk[:, 0:DH], x_mx[n // ROUND], n % ROUND, wq_mx)
-
-        def project_k(n):
-            project(qk_banks[n][:, DH : 2 * DH], x_mx[n // ROUND], n % ROUND, wk_mx)
-
-        def project_v(n):
-            r, i = divmod(n, ROUND)
-            if i == 0 and n < N_TILES - LAG:
-                v_tile = v_psum.tile([P, ROUND * DH], F32, name="v_bank")
-                v_banks[r] = v_tile[:]
-            elif i == 0 or r == ROUNDS - 1:
-                v_tile = xt_psum.tile([P, 4, P], F32, name="xt")
-                v_banks[r] = v_tile[:].rearrange("p a r -> p (a r)")
-            project(v_banks[r][:, i * DH : (i + 1) * DH], x_mx[r], i, wv_mx)
-            if r == ROUNDS - 1:
-                v_rows = v_pool.tile([P, ROUND * DH], F32, name="v_rows")
-                nc.scalar.copy(out=v_rows[:, 0:DH], in_=v_banks[r][:, i * DH : (i + 1) * DH])
-                store(out_2, r, i, v_rows[:, 0:DH])
-            elif i == ROUND - 1:
-                v_rows = v_pool.tile([P, ROUND * DH], F32, name="v_rows")
-                nc.scalar.copy(out=v_rows[:], in_=v_banks[r])
-                store(out_2, r, 0, v_rows[:])
-
-        def multiplies(n):
-            r, i = divmod(n, ROUND)
-            products[n] = multiply(qk_banks[n], first_tile_of(r) + i)
-
-        def subtract(engine, n):
-            r, i = divmod(n, ROUND)
-            if i == 0 or r == ROUNDS - 1:
-                rotated[r] = work.tile([P, 2, ROUND, DH], F32, name="rotated")
-            combine(engine, products[n], rotated[r][:, :, i, :])
-            if r == ROUNDS - 1:
-                store_qk(r, rotated[r], i, 1)
-            elif i == ROUND - 1:
-                store_qk(r, rotated[r], 0, ROUND)
-
-        transposes(0)
+        transpose(0)
         for g in range(PASSES - 1):
             regroup_w(vector_copy, wq_grouped, wq_raw, g)
         regroup_w(scalar_copy, wq_grouped, wq_raw, PASSES - 1)
         quantise_w(wq_mx, wq_grouped, 0)
-        quantise(0)
+        quantise_x(0)
         quantise_w(wq_mx, wq_grouped, 2)
-        transposes(1)
+        transpose(1)
         project_q(0)
         table_waves(0)
         regroup_w(vector_copy, wk_grouped, wk_raw, 0)
-        quantise(1)
+        quantise_x(1)
         for g in range(1, PASSES):
             regroup_w(vector_copy, wk_grouped, wk_raw, g)
         quantise_w(wk_mx, wk_grouped, 0)
         quantise_w(wk_mx, wk_grouped, 2)
-        transposes(2)
+        transpose(2)
         project_q(1)
-        quantise(2)
-        transposes(3)
+        quantise_x(2)
+        transpose(3)
         project_k(0)
         project_k(1)
         table_products(0)
-        quantise(3)
+        quantise_x(3)
         project_q(2)
         project_k(2)
-        multiplies(0)
-        wv_grouped = grouped_w()
+        multiply(0)
+        wv_grouped = new_w_grouped()
         regroup_w(scalar_copy, wv_grouped, wv_raw, 0)
         regroup_w(scalar_copy, wv_grouped, wv_raw, 1)
-        transposes(4)
-        multiplies(1)
+        transpose(4)
+        multiply(1)
         subtract(nc.gpsimd, 0)
         regroup_w(scalar_copy, wv_grouped, wv_raw, 2)
-        quantise(4)
+        quantise_x(4)
         regroup_w(vector_copy, wv_grouped, wv_raw, 3)
         subtract(nc.vector, 1)
         quantise_w(wv_mx, wv_grouped, 0)
         quantise_w(wv_mx, wv_grouped, 2)
 
-        for n in range(3, N_TILES + 1):
-            r, i = divmod(n, ROUND)
-            if n == N_TILES:
-                for late in range(N_TILES - LAG, N_TILES):
+        for n in range(3, ALL_TILES + 1):
+            t = first_tile_of(n // ROUND)
+            rotates = n % ROUND == 0 and n > 3
+            if n == ALL_TILES:
+                for late in range(ALL_TILES - LAG, ALL_TILES):
                     project_v(late)
-            new_tables = n % (2 * ROUND) == 0 and n < N_TILES
-            if n + 2 < N_TILES:
-                transposes(n + 2)
+            if n + AHEAD < ALL_TILES:
+                transpose(n + AHEAD)
                 if n == 3:
                     table_waves(ROUND)
-                elif n % (2 * ROUND) == 1 and first_tile_of(r) + ROUND < TILES:
-                    table_waves(first_tile_of(r) + ROUND)
-            if 4 <= n and n + 4 < N_TILES and n % 3 != 0:
-                x_words[n + 4] = permute_x(scalar_copy, x_raw[(n + 4) // ROUND], (n + 4) % ROUND)
-            if i == 0 and n - 1 >= 3 or n == N_TILES:
-                multiplies(n - 2)
-                multiplies(n - 1)
+                elif n % (BATCH * ROUND) == 1 and t + ROUND < TILES:
+                    table_waves(t + ROUND)
+            if 4 <= n < ALL_TILES - 4 and n % 3 != 0:
+                sort_words(n + 4)
+            if rotates:
+                multiply(n - 2)
+                multiply(n - 1)
                 subtract(nc.gpsimd, n - 2)
-            if n + 2 < N_TILES:
-                quantise(n + 2)
-            if new_tables:
-                table_products(first_tile_of(r))
-            if i == 0 and n - 1 >= 3 or n == N_TILES:
+            if n + AHEAD < ALL_TILES:
+                quantise_x(n + AHEAD)
+            if n % (BATCH * ROUND) == 0 and n < ALL_TILES:
+                table_products(t)
+            if rotates:
                 subtract(nc.vector, n - 1)
-            if n < N_TILES:
+            if n < ALL_TILES:
                 project_q(n)
                 project_k(n)
-            if LAG <= n < N_TILES:
+            if LAG <= n < ALL_TILES:
                 project_v(n - LAG)

@@ -114,7 +114,7 @@ def tile_retblock_pa_kernel(tc, x, w_q, w_k, w_v, out_0, out_1, out_2):
                 in_=words_of(n).rearrange("p (g w u) -> p g u w", g=PASSES, u=2),
             )
 
-        def transpose(n):
+        def transpose(n, between=None):
             if n % ROUND == 0:
                 x_mx[n // ROUND] = new_x_mx()
             x_grouped[n] = x_grouped_pool.tile([P, HID], BF16, align_bytes=64, name="x_grouped")
@@ -130,6 +130,8 @@ def tile_retblock_pa_kernel(tc, x, w_q, w_k, w_v, out_0, out_1, out_2):
                         column = words_of(n)[:, first + a % 2 : first + 2 * P : 2]
                     nc.tensor.transpose(xt[:, a, :], column, ident[:])
                 first = bank * 4 * P
+                if between:
+                    between(bank)
                 nc.scalar.copy(
                     out=grouped_words[:, first : first + 4 * P].rearrange(
                         "p (g r u) -> p g r u", g=2, u=2
@@ -237,8 +239,8 @@ def tile_retblock_pa_kernel(tc, x, w_q, w_k, w_v, out_0, out_1, out_2):
             for doubling in range(3, 7):
                 double(2**doubling)
 
-        def table_zoom():
-            for t in range(TILES):
+        def table_zoom(first, end):
+            for t in range(first, end):
                 for m in range(2):
                     nc.scalar.activation(
                         out=zoom[:, t, m, :], in_=log_base[:], func=ACT.Exp,
@@ -333,16 +335,18 @@ def tile_retblock_pa_kernel(tc, x, w_q, w_k, w_v, out_0, out_1, out_2):
         wq_raw, wk_raw, wv_raw = new_w_raw("wq_raw"), new_w_raw("wk_raw"), new_w_raw("wv_raw")
 
         load_x(0)
-        for g in range(PASSES):
-            load_w(w_q, wq_raw, g, g + 1)
         load_x(1)
-        load_w(w_k, wk_raw, 0, PASSES // 2)
+        load_w(w_q, wq_raw, 0, 1)
+        load_w(w_q, wq_raw, 1, 2)
+        load_w(w_q, wq_raw, 2, 3)
+        load_w(w_q, wq_raw, 3, 4)
         load_x(2)
-        load_w(w_k, wk_raw, PASSES // 2, PASSES)
+        load_w(w_k, wk_raw, 0, 2)
+        load_w(w_k, wk_raw, 2, 4)
         load_x(3)
-        load_w(w_v, wv_raw, 0, PASSES // 2)
-        load_w(w_v, wv_raw, PASSES // 2, PASSES)
+        load_w(w_v, wv_raw, 0, 2)
         load_x(4)
+        load_w(w_v, wv_raw, 2, 4)
         load_x(5)
         for n in range(6, ALL_TILES, ROUND):
             load_x(n, tiles=ROUND)
@@ -354,18 +358,18 @@ def tile_retblock_pa_kernel(tc, x, w_q, w_k, w_v, out_0, out_1, out_2):
         pos_turns = const.tile([P, TILES], F32, name="pos_turns")
         freq = const.tile([P, PAIRS], F32, name="freq")
         table_columns()
-        table_zoom()
         table_turns()
 
         wq_mx, wk_mx, wv_mx = new_w_mx("wq"), new_w_mx("wk"), new_w_mx("wv")
         wq_grouped, wk_grouped = new_w_grouped(), new_w_grouped()
         vector_copy, scalar_copy = nc.vector.tensor_copy, nc.scalar.copy
 
-        transpose(0)
+        transpose(0, lambda bank: table_zoom(4 * bank, 4 + bank))
+        table_zoom(5, TILES)
         for g in range(PASSES - 1):
             regroup_w(vector_copy, wq_grouped, wq_raw, g)
-        regroup_w(scalar_copy, wq_grouped, wq_raw, PASSES - 1)
         quantise_w(wq_mx, wq_grouped, 0)
+        regroup_w(vector_copy, wq_grouped, wq_raw, PASSES - 1)
         quantise_x(0)
         quantise_w(wq_mx, wq_grouped, 2)
         transpose(1)

@@ -38,7 +38,7 @@ def tile_retblock_pa_kernel(tc, x, w_q, w_k, w_v, out_0, out_1, out_2):
     with ExitStack() as ctx:
         const = ctx.enter_context(tc.tile_pool(name="const", bufs=1))
         x_raw_pool = ctx.enter_context(tc.tile_pool(name="x_raw_pool", bufs=ROUNDS))
-        x_sorted_pool = ctx.enter_context(tc.tile_pool(name="x_sorted_pool", bufs=2))
+        x_sorted_pool = ctx.enter_context(tc.tile_pool(name="x_sorted_pool", bufs=3))
         x_grouped_pool = ctx.enter_context(tc.tile_pool(name="x_grouped_pool", bufs=4))
         x_mx_pool = ctx.enter_context(tc.tile_pool(name="x_mx_pool", bufs=LAG // ROUND + 2))
         w_grouped_pool = ctx.enter_context(tc.tile_pool(name="w_grouped_pool", bufs=2))
@@ -107,9 +107,9 @@ def tile_retblock_pa_kernel(tc, x, w_q, w_k, w_v, out_0, out_1, out_2):
             r, i = divmod(n, ROUND)
             return x_raw[r][:].bitcast(F32)[:, i * WORDS : (i + 1) * WORDS]
 
-        def sort_words(n):
+        def sort_words(copy, n):
             x_sorted[n] = x_sorted_pool.tile([P, WORDS], F32, align_bytes=64, name="x_sorted")
-            nc.scalar.copy(
+            copy(
                 out=x_sorted[n][:].rearrange("p (g u w) -> p g u w", g=PASSES, u=2),
                 in_=words_of(n).rearrange("p (g w u) -> p g u w", g=PASSES, u=2),
             )
@@ -194,7 +194,7 @@ def tile_retblock_pa_kernel(tc, x, w_q, w_k, w_v, out_0, out_1, out_2):
                 nc.scalar.copy(
                     out=v_rows[:, 0:width], in_=v_banks[r][:, first * DH : first * DH + width]
                 )
-                store(out_2, r, first, v_rows[:, 0:width])
+                store(nc.scalar, out_2, r, first, v_rows[:, 0:width])
 
         plain = [P, TILES, PAIRS]
         both = [P, TILES, 2, PAIRS]
@@ -321,12 +321,12 @@ def tile_retblock_pa_kernel(tc, x, w_q, w_k, w_v, out_0, out_1, out_2):
                 first = i if last else 0
                 for m, out in ((0, out_0), (1, out_1)):
                     rows = rotated[r][:, m, first : i + 1].rearrange("p i d -> p (i d)")
-                    store(out, r, first, rows)
+                    store(nc.sync, out, r, first, rows)
 
-        def store(out, r, i, tile_rows):
+        def store(queue, out, r, i, tile_rows):
             rows = out[batch_of(r)].rearrange("(p t) d -> p (t d)", t=TILES)
             first = (first_tile_of(r) + i) * DH
-            nc.sync.dma_start(out=rows[:, first : first + tile_rows.shape[1]], in_=tile_rows)
+            queue.dma_start(out=rows[:, first : first + tile_rows.shape[1]], in_=tile_rows)
 
         x_raw, x_sorted, x_grouped, x_mx = {}, {}, {}, {}
         qk_banks, v_banks, terms, rotated = {}, {}, {}, {}
@@ -406,31 +406,32 @@ def tile_retblock_pa_kernel(tc, x, w_q, w_k, w_v, out_0, out_1, out_2):
         quantise_w(wv_mx, wv_grouped, 2)
 
         for n in range(3, ALL_TILES + 1):
-            t = first_tile_of(n // ROUND)
-            rotates = n % ROUND == 0 and n > 3
-            if n == ALL_TILES:
-                for late in range(ALL_TILES - LAG, ALL_TILES):
-                    project_v(late)
+            makes_tables = n % (BATCH * ROUND) == 3 and n < ALL_TILES - 1
+            next_pair = first_tile_of((n + 1) // ROUND)
             if n + AHEAD < ALL_TILES:
                 transpose(n + AHEAD)
-                if n == 3:
-                    table_waves(ROUND)
-                elif n % (BATCH * ROUND) == 1 and t + ROUND < TILES:
-                    table_waves(t + ROUND)
-            if 4 <= n < ALL_TILES - 4 and n % 3 != 0:
-                sort_words(n + 4)
-            if rotates:
-                multiply(n - 2)
-                multiply(n - 1)
+            if n == 3:
+                table_waves(next_pair)
+            elif n % (BATCH * ROUND) == 1 and next_pair + ROUND < TILES:
+                table_waves(next_pair + ROUND)
+            if n >= 4 and n + 4 < ALL_TILES and n % 4 != 3:
+                sort_words(scalar_copy, n + 4)
+            if makes_tables:
+                table_products(next_pair)
+                if 8 <= n + 4 < ALL_TILES:
+                    sort_words(vector_copy, n + 4)
+                if n >= 4:
+                    subtract(nc.vector, n - 2)
+            if 4 < n + 1 < ALL_TILES:
+                quantise_x(n + 1)
+            if n >= 4 and not makes_tables:
                 subtract(nc.gpsimd, n - 2)
-            if n + AHEAD < ALL_TILES:
-                quantise_x(n + AHEAD)
-            if n % (BATCH * ROUND) == 0 and n < ALL_TILES:
-                table_products(t)
-            if rotates:
-                subtract(nc.vector, n - 1)
+            multiply(n - 1)
             if n < ALL_TILES:
                 project_q(n)
                 project_k(n)
-            if LAG <= n < ALL_TILES:
-                project_v(n - LAG)
+                if n >= LAG:
+                    project_v(n - LAG)
+        subtract(nc.vector, ALL_TILES - 1)
+        for late in range(ALL_TILES - LAG, ALL_TILES):
+            project_v(late)

@@ -194,7 +194,7 @@ def tile_retblock_pa_kernel(tc, x, w_q, w_k, w_v, out_0, out_1, out_2):
                 nc.scalar.copy(
                     out=v_rows[:, 0:width], in_=v_banks[r][:, first * DH : first * DH + width]
                 )
-                store(nc.scalar, out_2, r, first, v_rows[:, 0:width])
+                store(out_2, r, first, v_rows[:, 0:width])
 
         plain = [P, TILES, PAIRS]
         both = [P, TILES, 2, PAIRS]
@@ -321,12 +321,12 @@ def tile_retblock_pa_kernel(tc, x, w_q, w_k, w_v, out_0, out_1, out_2):
                 first = i if last else 0
                 for m, out in ((0, out_0), (1, out_1)):
                     rows = rotated[r][:, m, first : i + 1].rearrange("p i d -> p (i d)")
-                    store(nc.sync, out, r, first, rows)
+                    store(out, r, first, rows)
 
-        def store(queue, out, r, i, tile_rows):
+        def store(out, r, i, tile_rows):
             rows = out[batch_of(r)].rearrange("(p t) d -> p (t d)", t=TILES)
             first = (first_tile_of(r) + i) * DH
-            queue.dma_start(out=rows[:, first : first + tile_rows.shape[1]], in_=tile_rows)
+            nc.sync.dma_start(out=rows[:, first : first + tile_rows.shape[1]], in_=tile_rows)
 
         x_raw, x_sorted, x_grouped, x_mx = {}, {}, {}, {}
         qk_banks, v_banks, terms, rotated = {}, {}, {}, {}
@@ -432,6 +432,7 @@ def tile_retblock_pa_kernel(tc, x, w_q, w_k, w_v, out_0, out_1, out_2):
                 project_k(n)
                 if n >= LAG:
                     project_v(n - LAG)
-        subtract(nc.vector, ALL_TILES - 1)
-        for late in range(ALL_TILES - LAG, ALL_TILES):
+        for late in range(ALL_TILES - LAG, ALL_TILES - 1):
             project_v(late)
+        subtract(nc.vector, ALL_TILES - 1)
+        project_v(ALL_TILES - 1)

@@ -22,6 +22,9 @@ PASSES = HID // (P * PACK)
 WORDS = HID // 2
 ROUND = 2
 ROUNDS = ALL_TILES // ROUND
+SINGLES = 3
+CAUGHT_UP = 8
+SHARE = 16
 AHEAD = 2
 LAG = 4
 
@@ -178,8 +181,8 @@ def tile_retblock_pa_kernel(tc, x, w_q, w_k, w_v, out_0, out_1, out_2):
 
         def project_v(n):
             r, i = divmod(n, ROUND)
-            last = r == ROUNDS - 1
-            if i == 0 or last:
+            single = r >= ROUNDS - SINGLES
+            if i == 0 or single:
                 if n < ALL_TILES - LAG:
                     v_banks[r] = v_psum.tile([P, ROUND * DH], F32, name="v_bank")[:]
                 else:
@@ -187,8 +190,8 @@ def tile_retblock_pa_kernel(tc, x, w_q, w_k, w_v, out_0, out_1, out_2):
                         "p a r -> p (a r)"
                     )
             project(v_banks[r][:, i * DH : (i + 1) * DH], n, wv_mx)
-            if last or i == ROUND - 1:
-                first = i if last else 0
+            if single or i == ROUND - 1:
+                first = i if single else 0
                 width = (i + 1 - first) * DH
                 v_rows = v_rows_pool.tile([P, ROUND * DH], F32, name="v_rows")
                 nc.scalar.copy(
@@ -305,20 +308,23 @@ def tile_retblock_pa_kernel(tc, x, w_q, w_k, w_v, out_0, out_1, out_2):
             nc.vector.tensor_tensor(out=crossed[:, 1, :], in0=y[:, :, 0], in1=sin_t, op=ALU.mult)
             terms[n] = straight, crossed
 
-        def subtract(engine, n):
+        def subtract(*parts):
+            n = len(subtracted)
+            subtracted.append(n)
             r, i = divmod(n, ROUND)
-            last = r == ROUNDS - 1
-            if i == 0 or last:
+            single = r >= ROUNDS - SINGLES
+            if i == 0 or single:
                 rotated[r] = work.tile([P, 2, ROUND, DH], F32, name="rotated")
             straight, crossed = terms[n]
-            engine.tensor_tensor(
-                out=rotated[r][:, :, i, :].rearrange("p m (j e) -> p m j e", e=2),
-                in0=crossed[:].rearrange("p e (m j) -> p m j e", m=2),
-                in1=straight[:].rearrange("p (m j) e -> p m j e", m=2),
-                op=ALU.subtract,
-            )
-            if last or i == ROUND - 1:
-                first = i if last else 0
+            for engine, pairs in parts:
+                engine.tensor_tensor(
+                    out=rotated[r][:, :, i].rearrange("p m (j e) -> p m j e", e=2)[:, :, pairs],
+                    in0=crossed[:].rearrange("p e (m j) -> p m j e", m=2)[:, :, pairs],
+                    in1=straight[:].rearrange("p (m j) e -> p m j e", m=2)[:, :, pairs],
+                    op=ALU.subtract,
+                )
+            if single or i == ROUND - 1:
+                first = i if single else 0
                 for m, out in ((0, out_0), (1, out_1)):
                     rows = rotated[r][:, m, first : i + 1].rearrange("p i d -> p (i d)")
                     store(out, r, first, rows)
@@ -329,24 +335,25 @@ def tile_retblock_pa_kernel(tc, x, w_q, w_k, w_v, out_0, out_1, out_2):
             nc.sync.dma_start(out=rows[:, first : first + tile_rows.shape[1]], in_=tile_rows)
 
         x_raw, x_sorted, x_grouped, x_mx = {}, {}, {}, {}
-        qk_banks, v_banks, terms, rotated = {}, {}, {}, {}
+        qk_banks, v_banks, terms, rotated, subtracted = {}, {}, {}, {}, []
+        by_vector, by_gpsimd = (nc.vector, slice(0, PAIRS)), (nc.gpsimd, slice(0, PAIRS))
         for r in range(ROUNDS):
             x_raw[r] = x_raw_pool.tile([P, ROUND * HID], BF16, name="x_raw")
         wq_raw, wk_raw, wv_raw = new_w_raw("wq_raw"), new_w_raw("wk_raw"), new_w_raw("wv_raw")
 
         load_x(0)
-        load_x(1)
         load_w(w_q, wq_raw, 0, 1)
         load_w(w_q, wq_raw, 1, 2)
+        load_x(1)
         load_w(w_q, wq_raw, 2, 3)
         load_w(w_q, wq_raw, 3, 4)
         load_x(2)
-        load_w(w_k, wk_raw, 0, 2)
-        load_w(w_k, wk_raw, 2, 4)
+        load_w(w_k, wk_raw, 0, PASSES // 2)
+        load_w(w_k, wk_raw, PASSES // 2, PASSES)
         load_x(3)
-        load_w(w_v, wv_raw, 0, 2)
+        load_w(w_v, wv_raw, 0, PASSES // 2)
         load_x(4)
-        load_w(w_v, wv_raw, 2, 4)
+        load_w(w_v, wv_raw, PASSES // 2, PASSES)
         load_x(5)
         for n in range(6, ALL_TILES, ROUND):
             load_x(n, tiles=ROUND)
@@ -375,6 +382,7 @@ def tile_retblock_pa_kernel(tc, x, w_q, w_k, w_v, out_0, out_1, out_2):
         transpose(1)
         project_q(0)
         table_waves(0)
+        table_waves(ROUND)
         regroup_w(vector_copy, wk_grouped, wk_raw, 0)
         quantise_x(1)
         for g in range(1, PASSES):
@@ -397,11 +405,11 @@ def tile_retblock_pa_kernel(tc, x, w_q, w_k, w_v, out_0, out_1, out_2):
         regroup_w(scalar_copy, wv_grouped, wv_raw, 1)
         transpose(4)
         multiply(1)
-        subtract(nc.gpsimd, 0)
+        subtract(by_gpsimd)
         regroup_w(scalar_copy, wv_grouped, wv_raw, 2)
         quantise_x(4)
         regroup_w(vector_copy, wv_grouped, wv_raw, 3)
-        subtract(nc.vector, 1)
+        subtract(by_vector)
         quantise_w(wv_mx, wv_grouped, 0)
         quantise_w(wv_mx, wv_grouped, 2)
 
@@ -410,9 +418,7 @@ def tile_retblock_pa_kernel(tc, x, w_q, w_k, w_v, out_0, out_1, out_2):
             next_pair = first_tile_of((n + 1) // ROUND)
             if n + AHEAD < ALL_TILES:
                 transpose(n + AHEAD)
-            if n == 3:
-                table_waves(next_pair)
-            elif n % (BATCH * ROUND) == 1 and next_pair + ROUND < TILES:
+            if n % (BATCH * ROUND) == 1 and next_pair + ROUND < TILES:
                 table_waves(next_pair + ROUND)
             if n >= 4 and n + 4 < ALL_TILES and n % 4 != 3:
                 sort_words(scalar_copy, n + 4)
@@ -420,13 +426,16 @@ def tile_retblock_pa_kernel(tc, x, w_q, w_k, w_v, out_0, out_1, out_2):
                 table_products(next_pair)
                 if 8 <= n + 4 < ALL_TILES:
                     sort_words(vector_copy, n + 4)
-                if n >= 4:
-                    subtract(nc.vector, n - 2)
+                if len(subtracted) < len(terms):
+                    subtract(
+                        (nc.vector, slice(0, SHARE + 1)), (nc.gpsimd, slice(SHARE, PAIRS))
+                    )
             if 4 < n + 1 < ALL_TILES:
                 quantise_x(n + 1)
-            if n >= 4 and not makes_tables:
-                subtract(nc.gpsimd, n - 2)
-            multiply(n - 1)
+            for tile in range(len(terms), n - 1 if n < CAUGHT_UP else n):
+                if len(subtracted) < len(terms):
+                    subtract(by_gpsimd)
+                multiply(tile)
             if n < ALL_TILES:
                 project_q(n)
                 project_k(n)
@@ -434,5 +443,5 @@ def tile_retblock_pa_kernel(tc, x, w_q, w_k, w_v, out_0, out_1, out_2):
                     project_v(n - LAG)
         for late in range(ALL_TILES - LAG, ALL_TILES - 1):
             project_v(late)
-        subtract(nc.vector, ALL_TILES - 1)
+        subtract(by_vector)
         project_v(ALL_TILES - 1)

@@ -23,7 +23,6 @@ WORDS = HID // 2
 ROUND = 2
 ROUNDS = ALL_TILES // ROUND
 SINGLES = 3
-CAUGHT_UP = 8
 SHARE = 16
 AHEAD = 2
 LAG = 4
@@ -432,10 +431,9 @@ def tile_retblock_pa_kernel(tc, x, w_q, w_k, w_v, out_0, out_1, out_2):
                     )
             if 4 < n + 1 < ALL_TILES:
                 quantise_x(n + 1)
-            for tile in range(len(terms), n - 1 if n < CAUGHT_UP else n):
-                if len(subtracted) < len(terms):
-                    subtract(by_gpsimd)
-                multiply(tile)
+            if len(subtracted) < len(terms):
+                subtract(by_gpsimd)
+            multiply(n - 1)
             if n < ALL_TILES:
                 project_q(n)
                 project_k(n)

from contextlib import ExitStack
import math

import concourse.mybir as mybir
from concourse.masks import make_identity

F32 = mybir.dt.float32
BF16 = mybir.dt.bfloat16
U32 = mybir.dt.uint32
U8 = mybir.dt.uint8
FP8X4 = mybir.dt.float8_e4m3fn_x4
ALU = mybir.AluOpType
ACT = mybir.ActivationFunctionType

P = 128
BATCH, SEQ, HID, DH = 2, 1024, 2048, 256
PAIRS = DH // 2
TILES = SEQ // P
ALL_TILES = BATCH * TILES
PACK = 4
PASSES = HID // (P * PACK)
WORDS = HID // 2
ROUND = 2
ROUNDS = ALL_TILES // ROUND
SINGLES = 3
SHARE = 16
AHEAD = 2
LAG = 4

ROTARY_BASE = 10000.0
SCALE_BASE = 512.0
FAST = math.ceil(PAIRS * math.log((SEQ - 1) / math.pi) / math.log(ROTARY_BASE))
ROUND_MAGIC = 1.5 * 2.0**23

FLOPS = 2 * BATCH * SEQ * HID * 3 * DH


def tile_retblock_pa_kernel(tc, x, w_q, w_k, w_v, out_0, out_1, out_2):
    nc = tc.nc
    with ExitStack() as ctx:
        const = ctx.enter_context(tc.tile_pool(name="const", bufs=1))
        x_raw_pool = ctx.enter_context(tc.tile_pool(name="x_raw_pool", bufs=ROUNDS))
        x_sorted_pool = ctx.enter_context(tc.tile_pool(name="x_sorted_pool", bufs=3))
        x_grouped_pool = ctx.enter_context(tc.tile_pool(name="x_grouped_pool", bufs=4))
        x_mx_pool = ctx.enter_context(tc.tile_pool(name="x_mx_pool", bufs=LAG // ROUND + 2))
        w_grouped_pool = ctx.enter_context(tc.tile_pool(name="w_grouped_pool", bufs=2))
        work = ctx.enter_context(tc.tile_pool(name="work", bufs=3))
        v_rows_pool = ctx.enter_context(tc.tile_pool(name="v_rows_pool", bufs=5))
        xt_psum = ctx.enter_context(tc.psum_pool(name="xt_psum", bufs=3))
        qk_psum = ctx.enter_context(tc.psum_pool(name="qk_psum", bufs=4))
        v_psum = ctx.enter_context(tc.psum_pool(name="v_psum", bufs=1))
        ctx.enter_context(tc.manual_schedule())

        def batch_of(r):
            return r % BATCH

        def first_tile_of(r):
            return (r // BATCH) * ROUND

        def new_x_raw():
            return x_raw_pool.tile([P, ROUND * HID], BF16, name="x_raw")

        def load_x(n, tiles=1):
            r, i = divmod(n, ROUND)
            rows = x[batch_of(r)].rearrange("(p t) k -> p (t k)", t=TILES)
            first = (first_tile_of(r) + i) * HID
            nc.sync.dma_start(
                out=x_raw[r][:, i * HID : (i + tiles) * HID],
                in_=rows[:, first : first + tiles * HID],
            )

        def new_w_raw(name):
            return const.tile([P, PASSES * PACK, DH], BF16, name=name)

        def load_w(w, w_raw, first, end):
            nc.sync.dma_start(
                out=w_raw[:, first * PACK : end * PACK].rearrange("p (g t) c -> p g (t c)", t=PACK),
                in_=w.rearrange("(g p t) c -> p g (t c)", p=P, t=PACK)[:, first:end],
            )

        def new_w_grouped():
            return w_grouped_pool.tile(
                [P, PASSES, DH, PACK], BF16, align_bytes=64, name="w_grouped"
            )

        def regroup_w(copy, w_grouped, w_raw, g):
            copy(
                out=w_grouped[:, g].rearrange("p (c i) t -> p c t i", i=4),
                in_=w_raw[:, g * PACK : (g + 1) * PACK, :].rearrange(
                    "p t (c i) -> p c t i", i=4
                ),
            )

        def new_w_mx(name):
            codes = const.tile([P, PASSES * DH], U32, align_bytes=64, name=name + "_codes")
            scales = const.tile([P, PASSES * DH], U8, align_bytes=64, name=name + "_scales")
            return codes, scales

        def quantise_w(w_mx, w_grouped, g):
            codes, scales = w_mx
            cols = slice(g * DH, (g + 2) * DH)
            nc.vector.quantize_mx(
                out=codes[:, cols].bitcast(FP8X4),
                scales=scales[:, cols],
                in_=w_grouped[:, g : g + 2].rearrange("p g c t -> p (g c t)"),
            )

        def words_of(n):
            r, i = divmod(n, ROUND)
            return x_raw[r][:].bitcast(F32)[:, i * WORDS : (i + 1) * WORDS]

        def sort_words(copy, n):
            x_sorted[n] = x_sorted_pool.tile([P, WORDS], F32, align_bytes=64, name="x_sorted")
            copy(
                out=x_sorted[n][:].rearrange("p (g u w) -> p g u w", g=PASSES, u=2),
                in_=words_of(n).rearrange("p (g w u) -> p g u w", g=PASSES, u=2),
            )

        def transpose(n, between=None):
            if n % ROUND == 0:
                x_mx[n // ROUND] = new_x_mx()
            x_grouped[n] = x_grouped_pool.tile([P, HID], BF16, align_bytes=64, name="x_grouped")
            grouped_words = x_grouped[n][:].bitcast(F32)
            for bank in range(WORDS // (4 * P)):
                xt = xt_psum.tile([P, 4, P], F32, name="xt")
                for a in range(4):
                    if n in x_sorted:
                        first = (bank * 4 + a) * P
                        column = x_sorted[n][:, first : first + P]
                    else:
                        first = (bank * 2 + a // 2) * 2 * P
                        column = words_of(n)[:, first + a % 2 : first + 2 * P : 2]
                    nc.tensor.transpose(xt[:, a, :], column, ident[:])
                first = bank * 4 * P
                if between:
                    between(bank)
                nc.scalar.copy(
                    out=grouped_words[:, first : first + 4 * P].rearrange(
                        "p (g r u) -> p g r u", g=2, u=2
                    ),
                    in_=xt[:].rearrange("p (g u) r -> p g r u", u=2),
                )

        def new_x_mx():
            codes = x_mx_pool.tile([P, ROUND * PASSES * P], U32, align_bytes=64, name="x_codes")
            scales = x_mx_pool.tile([P, ROUND * PASSES * P], U8, align_bytes=64, name="x_scales")
            return codes, scales

        def quantise_x(n):
            r, i = divmod(n, ROUND)
            codes, scales = x_mx[r]
            cols = slice(i * PASSES * P, (i + 1) * PASSES * P)
            nc.vector.quantize_mx(
                out=codes[:, cols].bitcast(FP8X4), scales=scales[:, cols], in_=x_grouped[n][:]
            )

        def project(out, n, w_mx):
            r, i = divmod(n, ROUND)
            x_codes, x_scales = x_mx[r]
            w_codes, w_scales = w_mx
            for g in range(PASSES):
                tokens = slice((i * PASSES + g) * P, (i * PASSES + g + 1) * P)
                features = slice(g * DH, (g + 1) * DH)
                nc.tensor.matmul_mx(
                    out=out,
                    lhsT=x_codes[:, tokens].bitcast(FP8X4),
                    lhsT_scale=x_scales[:, tokens],
                    rhs=w_codes[:, features].bitcast(FP8X4),
                    rhs_scale=w_scales[:, features],
                    start=(g == 0),
                    stop=(g == PASSES - 1),
                )

        def project_q(n):
            qk_banks[n] = qk_psum.tile([P, 2 * DH], F32, name="qk")
            project(qk_banks[n][:, 0:DH], n, wq_mx)

        def project_k(n):
            project(qk_banks[n][:, DH : 2 * DH], n, wk_mx)

        def project_v(n):
            r, i = divmod(n, ROUND)
            single = r >= ROUNDS - SINGLES
            if i == 0 or single:
                if n < ALL_TILES - LAG:
                    v_banks[r] = v_psum.tile([P, ROUND * DH], F32, name="v_bank")[:]
                else:
                    v_banks[r] = xt_psum.tile([P, 4, P], F32, name="xt")[:].rearrange(
                        "p a r -> p (a r)"
                    )
            project(v_banks[r][:, i * DH : (i + 1) * DH], n, wv_mx)
            if single or i == ROUND - 1:
                first = i if single else 0
                width = (i + 1 - first) * DH
                v_rows = v_rows_pool.tile([P, ROUND * DH], F32, name="v_rows")
                nc.scalar.copy(
                    out=v_rows[:, 0:width], in_=v_banks[r][:, first * DH : first * DH + width]
                )
                store(out_2, r, first, v_rows[:, 0:width])

        plain = [P, TILES, PAIRS]
        both = [P, TILES, 2, PAIRS]
        angle = const.tile(plain, F32, name="angle")
        zoom = const.tile(both, F32, name="zoom")
        sine = const.tile(plain, F32, name="sine")
        versine = const.tile(plain, F32, name="versine")
        cos_tab = const.tile(both, F32, name="cos_tab")
        sin_tab = const.tile(both, F32, name="sin_tab")

        def table_columns():
            iota_options = dict(base=0, allow_small_or_imprecise_dtypes=True)
            nc.gpsimd.iota(
                log_base[:], pattern=[[1, PAIRS]], channel_multiplier=0, **iota_options
            )
            nc.gpsimd.iota(pos[:], pattern=[[1, TILES]], channel_multiplier=TILES, **iota_options)
            make_identity(nc, ident[:])

            def double(width):
                nc.vector.tensor_scalar(
                    out=freq[:, width : 2 * width], in0=freq[:, 0:width],
                    scalar1=ROTARY_BASE ** (-width / PAIRS), scalar2=None, op0=ALU.mult,
                )

            nc.vector.memset(freq[:, 0:1], 1.0)
            nc.vector.tensor_scalar(
                out=log_base[:], in0=log_base[:], scalar1=2.0 / (1.4 * DH), scalar2=0.4 / 1.4,
                op0=ALU.mult, op1=ALU.add,
            )
            nc.scalar.activation(out=log_base[:], in_=log_base[:], func=ACT.Ln)
            double(1)
            for m, unit in ((0, 1.0 / SCALE_BASE), (1, -1.0 / SCALE_BASE)):
                nc.vector.tensor_scalar(
                    out=centred[:, m], in0=pos[:], scalar1=float(SEQ // 2), scalar2=unit,
                    op0=ALU.subtract, op1=ALU.mult,
                )
                double(2 ** (m + 1))
            nc.vector.tensor_scalar(
                out=pos_turns[:], in0=pos[:], scalar1=1.0 / (2.0 * math.pi), scalar2=None,
                op0=ALU.mult,
            )
            for doubling in range(3, 7):
                double(2**doubling)

        def table_zoom(first, end):
            for t in range(first, end):
                for m in range(2):
                    nc.scalar.activation(
                        out=zoom[:, t, m, :], in_=log_base[:], func=ACT.Exp,
                        scale=centred[:, m, t : t + 1],
                    )

        def table_turns():
            halves = (slice(0, TILES // 2), slice(TILES // 2, TILES))
            fast_angle, whole = angle[:, :, 0:FAST], versine[:, :, 0:FAST]
            for t in range(TILES):
                nc.vector.tensor_scalar(
                    out=angle[:, t], in0=freq[:], scalar1=pos_turns[:, t : t + 1], scalar2=None,
                    op0=ALU.mult,
                )
            for t in halves:
                nc.vector.tensor_scalar(
                    out=whole[:, t], in0=fast_angle[:, t], scalar1=ROUND_MAGIC,
                    scalar2=ROUND_MAGIC, op0=ALU.add, op1=ALU.subtract,
                )
            for t in halves:
                nc.vector.tensor_tensor(
                    out=fast_angle[:, t], in0=fast_angle[:, t], in1=whole[:, t], op=ALU.subtract
                )

        def table_waves(first_tile):
            t = slice(first_tile, first_tile + ROUND)
            nc.scalar.activation(out=versine[:, t], in_=angle[:, t], func=ACT.Sin, scale=math.pi)
            nc.scalar.activation(out=sine[:, t], in_=angle[:, t], func=ACT.Sin, scale=2.0 * math.pi)
            nc.scalar.activation(
                out=versine[:, t], in_=versine[:, t], func=ACT.Square, scale=math.sqrt(2.0)
            )

        def table_products(first_tile):
            t = slice(first_tile, first_tile + ROUND)
            for m in range(2):
                nc.vector.scalar_tensor_tensor(
                    out=cos_tab[:, t, m], in0=versine[:, t], scalar=1.0, in1=zoom[:, t, m],
                    op0=ALU.subtract, op1=ALU.mult,
                )
            nc.vector.tensor_tensor(
                out=sin_tab[:, t],
                in0=sine[:, t].unsqueeze(2).to_broadcast([P, ROUND, 2, PAIRS]),
                in1=zoom[:, t], op=ALU.mult,
            )

        def multiply(n):
            r, i = divmod(n, ROUND)
            t = first_tile_of(r) + i
            y = qk_banks[n][:].rearrange("p (mj e) -> p mj e", e=2)
            cos_t = cos_tab[:, t].rearrange("p m j -> p (m j)")
            sin_t = sin_tab[:, t].rearrange("p m j -> p (m j)")
            straight = work.tile([P, 2 * PAIRS, 2], F32, name="straight")
            nc.vector.tensor_tensor(
                out=straight[:], in0=y, in1=cos_t.unsqueeze(2).to_broadcast([P, 2 * PAIRS, 2]),
                op=ALU.mult,
            )
            crossed = work.tile([P, 2, 2 * PAIRS], F32, name="crossed")
            nc.vector.scalar_tensor_tensor(
                out=crossed[:, 0, :], in0=y[:, :, 1], scalar=-1.0, in1=sin_t,
                op0=ALU.mult, op1=ALU.mult,
            )
            nc.vector.tensor_tensor(out=crossed[:, 1, :], in0=y[:, :, 0], in1=sin_t, op=ALU.mult)
            terms[n] = straight, crossed

        def subtract(*parts):
            n = len(subtracted)
            subtracted.append(n)
            r, i = divmod(n, ROUND)
            single = r >= ROUNDS - SINGLES
            if i == 0 or single:
                rotated[r] = work.tile([P, 2, ROUND, DH], F32, name="rotated")
            straight, crossed = terms[n]
            for engine, pairs in parts:
                engine.tensor_tensor(
                    out=rotated[r][:, :, i].rearrange("p m (j e) -> p m j e", e=2)[:, :, pairs],
                    in0=crossed[:].rearrange("p e (m j) -> p m j e", m=2)[:, :, pairs],
                    in1=straight[:].rearrange("p (m j) e -> p m j e", m=2)[:, :, pairs],
                    op=ALU.subtract,
                )
            if single or i == ROUND - 1:
                first = i if single else 0
                for m, out in ((0, out_0), (1, out_1)):
                    rows = rotated[r][:, m, first : i + 1].rearrange("p i d -> p (i d)")
                    store(out, r, first, rows)

        def store(out, r, i, tile_rows):
            rows = out[batch_of(r)].rearrange("(p t) d -> p (t d)", t=TILES)
            first = (first_tile_of(r) + i) * DH
            nc.sync.dma_start(out=rows[:, first : first + tile_rows.shape[1]], in_=tile_rows)

        x_raw, x_sorted, x_grouped, x_mx = {}, {}, {}, {}
        qk_banks, v_banks, terms, rotated, subtracted = {}, {}, {}, {}, []
        by_vector, by_gpsimd = (nc.vector, slice(0, PAIRS)), (nc.gpsimd, slice(0, PAIRS))
        for r in range(ROUNDS):
            x_raw[r] = x_raw_pool.tile([P, ROUND * HID], BF16, name="x_raw")
        wq_raw, wk_raw, wv_raw = new_w_raw("wq_raw"), new_w_raw("wk_raw"), new_w_raw("wv_raw")

        load_x(0)
        load_w(w_q, wq_raw, 0, 1)
        load_w(w_q, wq_raw, 1, 2)
        load_x(1)
        load_w(w_q, wq_raw, 2, 3)
        load_w(w_q, wq_raw, 3, 4)
        load_x(2)
        load_w(w_k, wk_raw, 0, PASSES // 2)
        load_w(w_k, wk_raw, PASSES // 2, PASSES)
        load_x(3)
        load_w(w_v, wv_raw, 0, PASSES // 2)
        load_x(4)
        load_w(w_v, wv_raw, PASSES // 2, PASSES)
        load_x(5)
        for n in range(6, ALL_TILES, ROUND):
            load_x(n, tiles=ROUND)

        ident = const.tile([P, P], F32, name="ident")
        log_base = const.tile([P, PAIRS], F32, name="log_base")
        pos = const.tile([P, TILES], F32, name="pos")
        centred = const.tile([P, 2, TILES], F32, name="centred")
        pos_turns = const.tile([P, TILES], F32, name="pos_turns")
        freq = const.tile([P, PAIRS], F32, name="freq")
        table_columns()
        table_turns()

        wq_mx, wk_mx, wv_mx = new_w_mx("wq"), new_w_mx("wk"), new_w_mx("wv")
        wq_grouped, wk_grouped = new_w_grouped(), new_w_grouped()
        vector_copy, scalar_copy = nc.vector.tensor_copy, nc.scalar.copy

        transpose(0, lambda bank: table_zoom(4 * bank, 4 + bank))
        table_zoom(5, TILES)
        for g in range(PASSES - 1):
            regroup_w(vector_copy, wq_grouped, wq_raw, g)
        quantise_w(wq_mx, wq_grouped, 0)
        regroup_w(vector_copy, wq_grouped, wq_raw, PASSES - 1)
        quantise_x(0)
        quantise_w(wq_mx, wq_grouped, 2)
        transpose(1)
        project_q(0)
        table_waves(0)
        table_waves(ROUND)
        regroup_w(vector_copy, wk_grouped, wk_raw, 0)
        quantise_x(1)
        for g in range(1, PASSES):
            regroup_w(vector_copy, wk_grouped, wk_raw, g)
        quantise_w(wk_mx, wk_grouped, 0)
        quantise_w(wk_mx, wk_grouped, 2)
        transpose(2)
        project_q(1)
        quantise_x(2)
        transpose(3)
        project_k(0)
        project_k(1)
        table_products(0)
        quantise_x(3)
        project_q(2)
        project_k(2)
        multiply(0)
        wv_grouped = new_w_grouped()
        regroup_w(scalar_copy, wv_grouped, wv_raw, 0)
        regroup_w(scalar_copy, wv_grouped, wv_raw, 1)
        transpose(4)
        multiply(1)
        subtract(by_gpsimd)
        regroup_w(scalar_copy, wv_grouped, wv_raw, 2)
        quantise_x(4)
        regroup_w(vector_copy, wv_grouped, wv_raw, 3)
        subtract(by_vector)
        quantise_w(wv_mx, wv_grouped, 0)
        quantise_w(wv_mx, wv_grouped, 2)

        for n in range(3, ALL_TILES + 1):
            makes_tables = n % (BATCH * ROUND) == 3 and n < ALL_TILES - 1
            next_pair = first_tile_of((n + 1) // ROUND)
            if n + AHEAD < ALL_TILES:
                transpose(n + AHEAD)
            if n % (BATCH * ROUND) == 1 and next_pair + ROUND < TILES:
                table_waves(next_pair + ROUND)
            if n >= 4 and n + 4 < ALL_TILES and n % 4 != 3:
                sort_words(scalar_copy, n + 4)
            if makes_tables:
                table_products(next_pair)
                if 8 <= n + 4 < ALL_TILES:
                    sort_words(vector_copy, n + 4)
                if len(subtracted) < len(terms):
                    subtract(
                        (nc.vector, slice(0, SHARE + 1)), (nc.gpsimd, slice(SHARE, PAIRS))
                    )
            if 4 < n + 1 < ALL_TILES:
                quantise_x(n + 1)
            if len(subtracted) < len(terms):
                subtract(by_gpsimd)
            multiply(n - 1)
            if n < ALL_TILES:
                project_q(n)
                project_k(n)
                if n >= LAG:
                    project_v(n - LAG)
        for late in range(ALL_TILES - LAG, ALL_TILES - 1):
            project_v(late)
        subtract(by_vector)
        project_v(ALL_TILES - 1)
